import numpy as np
import ml_dtypes


def mxq(x, axis, fmt="e4m3"):
    dtype, down = {"e4m3": (ml_dtypes.float8_e4m3fn, 7), "e5m2": (ml_dtypes.float8_e5m2, 14)}[fmt]
    v = np.moveaxis(np.asarray(x, np.float32).astype(ml_dtypes.bfloat16).astype(np.float64), axis, -1)
    blocks = v.reshape(v.shape[:-1] + (-1, 32))
    amax = np.abs(blocks).max(-1, keepdims=True)
    byte = np.maximum(np.where(amax > 0, np.frexp(amax)[1] - 1 + 127, 0) - down, 1)
    scale = np.exp2(byte - 127.0)
    codes = (blocks / scale).astype(np.float32).astype(dtype).astype(np.float64)
    return np.moveaxis((codes * scale).reshape(v.shape), -1, axis)


WIDE = False


def mx_kscale(k):
    if not WIDE:
        return np.ones(k)
    levels = np.array([30, -30])
    if k % 512:
        return np.exp2(np.random.permutation(np.resize(levels, k // 32))).repeat(32)
    a = np.empty((k // 512, 16))
    for p in range(k // 512):
        a[p, :8] = np.random.permutation(np.resize(levels, 8))
        for g in range(8):
            far = levels[np.abs(levels - a[p, g]) >= 10]
            a[p, g + 8] = far[np.random.randint(len(far))]
    return np.exp2(a.ravel()).repeat(32)


BF16 = ml_dtypes.bfloat16


def bf(x):
    return np.asarray(x, np.float32).astype(BF16)


def f64(x):
    return np.asarray(x).astype(np.float64)


B, S, H, NH, HD, ROT = 2, 512, 1024, 8, 128, 32
BASE = 10000.0


def rotate_half(x):
    half = x.shape[-1] // 2
    return np.concatenate((-x[..., half:], x[..., :half]), axis=-1)


def rope_tables(seq_len):
    inv_freq = 1.0 / (BASE ** (np.arange(0, ROT, 2) / ROT))
    freqs = np.arange(seq_len)[:, None] * inv_freq[None, :]
    emb = np.concatenate((freqs, freqs), axis=-1)
    return np.cos(emb), np.sin(emb)


def setup_inputs():
    s = mx_kscale(H)
    return {"hidden_states": bf(np.random.standard_normal((B, S, H)) * s),
            "W_qkv": bf(np.random.standard_normal((H, 3 * H)) / np.sqrt(H) / s[:, None]),
            "b_qkv": bf(np.random.standard_normal(3 * H) * 0.3)}


def reference(hidden_states, W_qkv, b_qkv):
    qkv = (mxq(f64(hidden_states), 2, "e5m2") @ mxq(f64(W_qkv), 0, "e4m3")) + f64(b_qkv)
    qkv = qkv.reshape(B, S, NH, 3 * HD)
    q = qkv[..., :HD].transpose(0, 2, 1, 3)
    k = qkv[..., HD:2 * HD].transpose(0, 2, 1, 3)
    v = qkv[..., 2 * HD:].transpose(0, 2, 1, 3)
    cos, sin = rope_tables(S)
    q_rot, q_pass = q[..., :ROT], q[..., ROT:]
    k_rot, k_pass = k[..., :ROT], k[..., ROT:]
    q_rot = q_rot * cos + rotate_half(q_rot) * sin
    k_rot = k_rot * cos + rotate_half(k_rot) * sin
    q = np.concatenate((q_rot, q_pass), axis=-1)
    k = np.concatenate((k_rot, k_pass), axis=-1)
    return q, k, np.ascontiguousarray(v)

@@ -1,0 +1,325 @@
+import math
+from contextlib import ExitStack
+
+import concourse.mybir as mybir
+from concourse.masks import make_identity
+
+B, S, H, NH, HD, ROT = 2, 512, 1024, 8, 128, 32
+BASE = 10000.0
+FLOPS = 2 * B * S * H * 3 * H
+
+F32 = mybir.dt.float32
+BF16 = mybir.dt.bfloat16
+I32 = mybir.dt.int32
+U32 = mybir.dt.uint32
+U8 = mybir.dt.uint8
+E4M3 = mybir.dt.float8_e4m3fn_x4
+E5M2 = mybir.dt.float8_e5m2_x4
+ALU = mybir.AluOpType
+ACT = mybir.ActivationFunctionType
+
+P = 128
+PACK = 4
+PASSES = H // (P * PACK)
+TT = S // P
+PAIRS = NH // 2
+PAIR_COLS = 2 * 3 * HD
+HALF = ROT // 2
+REST = HD - ROT
+STEPS = PAIRS * B
+
+
+def tile_pgtattention_pa_kernel(tc, hidden_states, W_qkv, b_qkv, out_0, out_1, out_2):
+    nc = tc.nc
+    outs = (out_0, out_1, out_2)
+
+    with ExitStack() as ctx:
+        keep = ctx.enter_context(tc.tile_pool(name="keep", bufs=1))
+        work = ctx.enter_context(tc.tile_pool(name="work", bufs=3))
+        psum = ctx.enter_context(tc.psum_pool(name="psum", bufs=1))
+        ctx.enter_context(tc.manual_schedule())
+
+        def bank(shape, dtype):
+            return psum.tile(shape, dtype, name="bank", tag="bank", bufs=6)
+
+        b_rows = keep.tile([P, PAIR_COLS], BF16)
+        nc.vector.memset(b_rows[:], 0.0)
+        nc.scalar.dma_start(out=b_rows[0:PAIRS, :], in_=b_qkv.rearrange("(r c) -> r c", r=PAIRS))
+        w_raw = {}
+        x_raw = {}
+
+        def load_w(pair):
+            for g in range(PASSES):
+                w_raw[pair, g] = keep.tile([P, PACK, PAIR_COLS], BF16, name="w_raw_%d_%d" % (pair, g))
+                rows = W_qkv[g * P * PACK:(g + 1) * P * PACK, pair * PAIR_COLS:(pair + 1) * PAIR_COLS]
+                nc.sync.dma_start(out=w_raw[pair, g][:], in_=rows.rearrange("(p j) c -> p j c", j=PACK))
+
+        load_w(0)
+        x_rows = [hidden_states[b].rearrange("(m t) k -> m t k", t=TT) for b in range(B)]
+        for t in range(TT):
+            tile_x = keep.tile([P, H], BF16, name="x_raw_0_%d" % t)
+            nc.sync.dma_start(out=tile_x[:], in_=x_rows[0][:, t, :])
+            x_raw[0, t] = tile_x[:]
+        x_raw_1 = keep.tile([P, TT, H], BF16)
+        nc.sync.dma_start(out=x_raw_1[:], in_=x_rows[1])
+        for t in range(TT):
+            x_raw[1, t] = x_raw_1[:, t, :]
+        for pair in range(1, PAIRS):
+            load_w(pair)
+
+
+        ident = keep.tile([P, P], F32)
+        make_identity(nc, ident[:])
+        pos = keep.tile([P, S], F32)
+        nc.gpsimd.iota(pos[:], pattern=[[1, TT], [TT, P]], base=0, channel_multiplier=0,
+                       allow_small_or_imprecise_dtypes=True)
+        pick = keep.tile([P, PAIRS], BF16)
+        nc.gpsimd.tensor_copy(out=pick[:], in_=ident[:, 0:PAIRS])
+        swap = keep.tile([P, P], F32)
+        ident_h = ident[:].rearrange("p (j f i) -> p j f i", f=2, i=HALF)
+        swap_h = swap[:].rearrange("p (j f i) -> p j f i", f=2, i=HALF)
+        for f in range(2):
+            nc.gpsimd.tensor_copy(out=swap_h[:, :, f, :], in_=ident_h[:, :, 1 - f, :])
+        b_rot_rows = keep.tile([P, P], BF16)
+        nc.gpsimd.tensor_copy(
+            out=b_rot_rows[:].rearrange("p (r h c) -> p r h c", r=2, h=2),
+            in_=b_rows[:].rearrange("p (h r c) -> p r h c", h=2, r=3)[:, 0:2, :, 0:ROT])
+
+        signs = keep.tile([P, 2], F32)
+        nc.vector.memset(signs[:, 0:1], 1.0)
+        nc.vector.memset(signs[:, 1:2], -1.0)
+        turns_row = keep.tile([P, 2, HALF], F32)
+        for i in range(HALF):
+            nc.vector.tensor_scalar(out=turns_row[:, :, i], in0=signs[:], scalar1=BASE ** (-i / HALF) / (2 * math.pi),
+                                    scalar2=None, op0=ALU.mult)
+        turns_diag = keep.tile([P, P // ROT, ROT], F32)
+        turns = keep.tile([P, 1], F32)
+        nc.vector.scalar_tensor_tensor(
+            out=turns_diag[:], in0=ident[:].rearrange("p (j c) -> p j c", c=ROT), scalar=1.0,
+            in1=turns_row[:].rearrange("p f i -> p (f i)").unsqueeze(1).to_broadcast([P, P // ROT, ROT]),
+            op0=ALU.mult, op1=ALU.mult, accum_out=turns[:])
+        whole_sin = keep.tile([P, S], I32)
+        whole_cos = keep.tile([P, S], I32)
+        frac_sin = keep.tile([P, S], F32)
+        frac_cos = keep.tile([P, S], F32)
+        nc.vector.tensor_scalar(out=whole_sin[:], in0=pos[:], scalar1=turns[:], scalar2=None, op0=ALU.mult)
+        nc.vector.tensor_scalar(out=whole_cos[:], in0=pos[:], scalar1=turns[:], scalar2=0.25, op0=ALU.mult, op1=ALU.add)
+        nc.vector.scalar_tensor_tensor(out=frac_sin[:], in0=pos[:], scalar=turns[:], in1=whole_sin[:],
+                                       op0=ALU.mult, op1=ALU.subtract)
+        nc.vector.scalar_tensor_tensor(out=frac_cos[:], in0=pos[:], scalar=turns[:], in1=whole_cos[:],
+                                       op0=ALU.mult, op1=ALU.subtract)
+        sin_t = keep.tile([P, S], F32)
+        cos_t = keep.tile([P, S], F32)
+        nc.scalar.activation(out=sin_t[:], in_=frac_sin[:], func=ACT.Sin, scale=2 * math.pi)
+        nc.scalar.activation(out=cos_t[:], in_=frac_cos[:], func=ACT.Sin, scale=2 * math.pi, bias=math.pi / 2)
+
+        b_all = []
+        for pair in range(PAIRS):
+            spread = bank([P, PAIR_COLS], BF16)
+            for c0 in range(0, PAIR_COLS, 512):
+                cols = slice(c0, min(c0 + 512, PAIR_COLS))
+                nc.tensor.matmul(spread[:, cols], lhsT=pick[:, pair:pair + 1].to_broadcast([P, P]),
+                                 rhs=b_rows[:, cols], start=True, stop=True)
+            b_pair = keep.tile([P, PAIR_COLS], BF16, name="b_pair_%d" % pair)
+            nc.scalar.copy(out=b_pair[:], in_=spread[:])
+            b_all.append(b_pair[:].rearrange("p (h r c) -> p r h c", h=2, r=3))
+        b_rot_ps = bank([P, PAIRS], F32)
+        nc.tensor.matmul(b_rot_ps[:], lhsT=b_rot_rows[:], rhs=pick[:], start=True, stop=True)
+        b_rot = keep.tile([P, PAIRS], F32)
+        nc.scalar.copy(out=b_rot[:], in_=b_rot_ps[:])
+
+        widths = {"rot": 4 * ROT, "rest": 4 * REST, "v": 2 * HD}
+        w_side = {}
+        w_codes = {}
+        w_scales = {}
+
+        def interleave(copy, pair, g, piece):
+            side = work.tile([P, widths[piece] * PACK], BF16, name="side_" + piece, align_bytes=64)
+            w_side[pair, g, piece] = side
+            src = w_raw[pair, g][:].rearrange("p j (h r c) -> p r h c j", h=2, r=3)
+            if piece == "rot":
+                copy(out=side[:].rearrange("p (r h c j) -> p r h c j", r=2, h=2, j=PACK), in_=src[:, 0:2, :, 0:ROT, :])
+                return
+            parts = [src[:, 2]] if piece == "v" else [src[:, r, :, ROT:HD, :] for r in range(2)]
+            dst = side[:].rearrange("p (r h c i j) -> p r h c j i", r=len(parts), h=2, i=4, j=PACK)
+            for r, part in enumerate(parts):
+                copy(out=dst[:, r], in_=part.rearrange("p h (c i) j -> p h c j i", i=4))
+
+        def quantize_w(pair, g, piece):
+            key = (pair, g, piece)
+            w_codes[key] = keep.tile([P, widths[piece]], U32, name="w_codes_%d_%d_%s" % key, align_bytes=64)
+            w_scales[key] = keep.tile([P, widths[piece]], U8, name="w_scales_%d_%d_%s" % key, align_bytes=64)
+            nc.vector.quantize_mx(out=w_codes[key][:].bitcast(E4M3), scales=w_scales[key][:], in_=w_side[key][:])
+
+        x_side = {}
+        x_codes = {}
+        x_scales = {}
+        for b in range(B):
+            for g in range(PASSES):
+                x_codes[b, g] = keep.tile([P, S], U32, name="x_codes_%d_%d" % (b, g), align_bytes=64)
+                x_scales[b, g] = keep.tile([P, S], U8, name="x_scales_%d_%d" % (b, g), align_bytes=64)
+
+        def transpose_x(b, t):
+            words = x_raw[b, t].bitcast(F32)
+            turned = bank([P, PASSES, 2, P], F32)
+            for g in range(PASSES):
+                for u in range(2):
+                    nc.tensor.transpose(turned[:, g, u, :], words[:, 2 * P * g + u:2 * P * (g + 1):2], ident[:])
+            side = work.tile([P, PASSES, P * PACK], BF16, name="side_x", bufs=4, align_bytes=64)
+            x_side[b, t] = side
+            nc.scalar.copy(out=side[:].bitcast(F32).rearrange("p g (m u) -> p g m u", u=2),
+                           in_=turned[:].rearrange("p g u m -> p g m u"))
+
+        def quantize_x(b, t):
+            cols = slice(t * P, (t + 1) * P)
+            for g in range(PASSES):
+                nc.vector.quantize_mx(out=x_codes[b, g][:, cols].bitcast(E5M2), scales=x_scales[b, g][:, cols],
+                                      in_=x_side[b, t][:, g, :])
+
+        def product(out, b, t, pair, piece, cols):
+            toks = slice(t * P, (t + 1) * P)
+            for g in range(PASSES):
+                key = (pair, g, piece)
+                nc.tensor.matmul_mx(
+                    out=out, lhsT=x_codes[b, g][:, toks].bitcast(E5M2), lhsT_scale=x_scales[b, g][:, toks],
+                    rhs=w_codes[key][:, cols].bitcast(E4M3), rhs_scale=w_scales[key][:, cols],
+                    start=(g == 0), stop=(g == PASSES - 1))
+
+        qk_stage = {}
+        v_stage = {}
+        terms = {}
+
+        def open_step(s):
+            qk_stage[s] = work.tile([P, 2, 2, TT, HD], F32, name="qk_stage", bufs=5)
+            v_stage[s] = work.tile([P, 2, TT, HD], F32, name="v_stage", bufs=5)
+
+        def rest_tile(s, t):
+            pair, b = divmod(s, B)
+            acc = bank([P, 4 * REST], F32)
+            product(acc[:, 0:256], b, t, pair, "rest", slice(0, 256))
+            product(acc[:, 256:384], b, t, pair, "rest", slice(256, 384))
+            nc.vector.tensor_tensor(out=qk_stage[s][:, :, :, t, ROT:HD],
+                                    in0=acc[:].rearrange("p (r h c) -> p r h c", r=2, h=2),
+                                    in1=b_all[pair][:, 0:2, :, ROT:HD], op=ALU.add)
+
+        def v_tiles(s, t0):
+            pair, b = divmod(s, B)
+            acc = bank([P, 2, 2 * HD], F32)
+            for dt in range(2):
+                product(acc[:, dt, :], b, t0 + dt, pair, "v", slice(0, 2 * HD))
+            nc.vector.tensor_tensor(out=v_stage[s][:, :, t0:t0 + 2, :].rearrange("p h t c -> p t h c"),
+                                    in0=acc[:].rearrange("p t (h c) -> p t h c", h=2),
+                                    in1=b_all[pair][:, 2].unsqueeze(1).to_broadcast([P, 2, 2, HD]), op=ALU.add)
+
+        rot_acc = {}
+
+        def rot_product(s):
+            pair, b = divmod(s, B)
+            acc = psum.tile([P, S], F32, name="rot_acc")
+            rot_acc[s] = acc
+            for g in range(PASSES):
+                key = (pair, g, "rot")
+                nc.tensor.matmul_mx(
+                    out=acc[:], lhsT=w_codes[key][:].bitcast(E4M3), lhsT_scale=w_scales[key][:],
+                    rhs=x_codes[b, g][:].bitcast(E5M2), rhs_scale=x_scales[b, g][:],
+                    start=(g == 0), stop=(g == PASSES - 1))
+
+        def rot_terms(s):
+            pair = s // B
+            by_cos = work.tile([P, S], F32, name="by_cos", bufs=2)
+            by_sin = work.tile([P, S], F32, name="by_sin", bufs=2)
+            terms[s] = (by_cos, by_sin)
+            for term, table in ((by_cos, cos_t), (by_sin, sin_t)):
+                nc.vector.scalar_tensor_tensor(out=term[:], in0=rot_acc[s][:], scalar=b_rot[:, pair:pair + 1],
+                                               in1=table[:], op0=ALU.add, op1=ALU.mult)
+
+        def rot_finish(s):
+            by_cos, by_sin = terms[s]
+            turned = psum.tile([P, TT, P], F32, name="rot_turned")
+            for t in range(TT):
+                toks = slice(t * P, (t + 1) * P)
+                nc.tensor.matmul(turned[:, t, :], lhsT=by_cos[:, toks], rhs=ident[:], start=True, stop=False,
+                                 is_transpose=True)
+                nc.tensor.matmul(turned[:, t, :], lhsT=by_sin[:, toks], rhs=swap[:], start=False, stop=True,
+                                 is_transpose=True)
+            nc.scalar.copy(out=qk_stage[s][:, :, :, :, 0:ROT].rearrange("p r h t c -> p (r h) t c"),
+                           in_=turned[:].rearrange("p t (j c) -> p j t c", c=ROT))
+
+        def store(s, r):
+            pair, b = divmod(s, B)
+            src = v_stage[s][:] if r == 2 else qk_stage[s][:, r]
+            dst = outs[r][b, 2 * pair:2 * pair + 2].rearrange("h (m t) c -> m h (t c)", t=TT)
+            nc.sync.dma_start(out=dst, in_=src.rearrange("p h t c -> p h (t c)"))
+
+        for g in range(PASSES):
+            interleave(nc.vector.tensor_copy, 0, g, "rest")
+            interleave(nc.vector.tensor_copy, 0, g, "rot")
+        for piece in ("rest", "rot"):
+            for g in range(PASSES):
+                quantize_w(0, g, piece)
+        for t in range(TT):
+            transpose_x(0, t)
+        for g in range(PASSES):
+            interleave(nc.scalar.copy, 0, g, "v")
+        open_step(0)
+        quantize_x(0, 0)
+        quantize_x(0, 1)
+        rest_tile(0, 0)
+        quantize_x(0, 2)
+        quantize_x(0, 3)
+        rest_tile(0, 1)
+        rot_product(0)
+        rest_tile(0, 2)
+        for g in range(PASSES):
+            quantize_w(0, g, "v")
+        rot_terms(0)
+        rest_tile(0, 3)
+        for t in range(TT):
+            transpose_x(1, t)
+        v_tiles(0, 0)
+        rot_finish(0)
+        store(0, 0)
+        store(0, 1)
+        v_tiles(0, 2)
+        store(0, 2)
+        for t in range(TT):
+            quantize_x(1, t)
+        rot_product(1)
+        for piece in ("rot", "rest"):
+            for g in range(PASSES):
+                interleave(nc.scalar.copy, 1, g, piece)
+
+        for s in range(1, STEPS):
+            pair, b = divmod(s, B)
+            more = pair + 1 < PAIRS
+            open_step(s)
+            rest_tile(s, 0)
+            if s == 1:
+                rot_terms(1)
+            rest_tile(s, 1)
+            rot_finish(s)
+            if more and b == 0:
+                for piece in ("rot", "rest"):
+                    for g in range(PASSES):
+                        interleave(nc.scalar.copy, pair + 1, g, piece)
+            if more and b == 1:
+                for g in range(PASSES):
+                    interleave(nc.scalar.copy, pair + 1, g, "v")
+            for g in range(PASSES):
+                if b == 0:
+                    quantize_w(pair, g, "v")
+                elif more:
+                    quantize_w(pair + 1, g, "rot")
+            rest_tile(s, 2)
+            rest_tile(s, 3)
+            store(s, 0)
+            store(s, 1)
+            if s + 1 < STEPS:
+                rot_product(s + 1)
+                if b == 1:
+                    for g in range(PASSES):
+                        quantize_w(pair + 1, g, "rest")
+                rot_terms(s + 1)
+            v_tiles(s, 0)
+            v_tiles(s, 2)
+            store(s, 2)

@@ -40,30 +40,30 @@ def tile_pgtattention_pa_kernel(tc, hidden_states, W_qkv, b_qkv, out_0, out_1, o
         ctx.enter_context(tc.manual_schedule())
 
         def bank(shape, dtype):
-            return psum.tile(shape, dtype, name="bank", tag="bank", bufs=6)
+            return psum.tile(shape, dtype, name="bank", tag="bank", bufs=8)
 
-        b_rows = keep.tile([P, PAIR_COLS], BF16)
-        nc.vector.memset(b_rows[:], 0.0)
-        nc.scalar.dma_start(out=b_rows[0:PAIRS, :], in_=b_qkv.rearrange("(r c) -> r c", r=PAIRS))
+        b_raw = keep.tile([PAIRS, PAIR_COLS], BF16)
+        nc.sync.dma_start(out=b_raw[:], in_=b_qkv.rearrange("(r c) -> r c", r=PAIRS))
         w_raw = {}
         x_raw = {}
 
-        def load_w(pair):
-            for g in range(PASSES):
+        def load_w(pair, passes=range(PASSES)):
+            for g in passes:
                 w_raw[pair, g] = keep.tile([P, PACK, PAIR_COLS], BF16, name="w_raw_%d_%d" % (pair, g))
                 rows = W_qkv[g * P * PACK:(g + 1) * P * PACK, pair * PAIR_COLS:(pair + 1) * PAIR_COLS]
                 nc.sync.dma_start(out=w_raw[pair, g][:], in_=rows.rearrange("(p j) c -> p j c", j=PACK))
 
-        load_w(0)
         x_rows = [hidden_states[b].rearrange("(m t) k -> m t k", t=TT) for b in range(B)]
-        for t in range(TT):
-            tile_x = keep.tile([P, H], BF16, name="x_raw_0_%d" % t)
-            nc.sync.dma_start(out=tile_x[:], in_=x_rows[0][:, t, :])
-            x_raw[0, t] = tile_x[:]
-        x_raw_1 = keep.tile([P, TT, H], BF16)
-        nc.sync.dma_start(out=x_raw_1[:], in_=x_rows[1])
-        for t in range(TT):
-            x_raw[1, t] = x_raw_1[:, t, :]
+
+        def load_x(b, t):
+            tile_x = keep.tile([P, H], BF16, name="x_raw_%d_%d" % (b, t))
+            nc.sync.dma_start(out=tile_x[:], in_=x_rows[b][:, t, :])
+            x_raw[b, t] = tile_x[:]
+
+        load_w(0)
+        for b in range(B):
+            for t in range(TT):
+                load_x(b, t)
         for pair in range(1, PAIRS):
             load_w(pair)
 
@@ -74,30 +74,34 @@ def tile_pgtattention_pa_kernel(tc, hidden_states, W_qkv, b_qkv, out_0, out_1, o
         nc.gpsimd.iota(pos[:], pattern=[[1, TT], [TT, P]], base=0, channel_multiplier=0,
                        allow_small_or_imprecise_dtypes=True)
         pick = keep.tile([P, PAIRS], BF16)
-        nc.gpsimd.tensor_copy(out=pick[:], in_=ident[:, 0:PAIRS])
+        nc.scalar.copy(out=pick[:], in_=ident[:, 0:PAIRS])
         swap = keep.tile([P, P], F32)
         ident_h = ident[:].rearrange("p (j f i) -> p j f i", f=2, i=HALF)
         swap_h = swap[:].rearrange("p (j f i) -> p j f i", f=2, i=HALF)
         for f in range(2):
-            nc.gpsimd.tensor_copy(out=swap_h[:, :, f, :], in_=ident_h[:, :, 1 - f, :])
+            nc.scalar.copy(out=swap_h[:, :, f, :], in_=ident_h[:, :, 1 - f, :])
+        b_rows = keep.tile([P, PAIR_COLS], BF16)
         b_rot_rows = keep.tile([P, P], BF16)
-        nc.gpsimd.tensor_copy(
-            out=b_rot_rows[:].rearrange("p (r h c) -> p r h c", r=2, h=2),
-            in_=b_rows[:].rearrange("p (h r c) -> p r h c", h=2, r=3)[:, 0:2, :, 0:ROT])
+        nc.vector.memset(b_rows[:], 0.0)
+        nc.vector.memset(b_rot_rows[:], 0.0)
 
-        signs = keep.tile([P, 2], F32)
-        nc.vector.memset(signs[:, 0:1], 1.0)
-        nc.vector.memset(signs[:, 1:2], -1.0)
+        one = keep.tile([P, 1], F32)
+        nc.vector.memset(one[:], 1.0)
         turns_row = keep.tile([P, 2, HALF], F32)
         for i in range(HALF):
-            nc.vector.tensor_scalar(out=turns_row[:, :, i], in0=signs[:], scalar1=BASE ** (-i / HALF) / (2 * math.pi),
+            nc.vector.tensor_scalar(out=turns_row[:, 0, i:i + 1], in0=one[:], scalar1=BASE ** (-i / HALF) / (2 * math.pi),
                                     scalar2=None, op0=ALU.mult)
+        nc.vector.tensor_scalar(out=turns_row[:, 1, :], in0=turns_row[:, 0, :], scalar1=-1.0, scalar2=None, op0=ALU.mult)
         turns_diag = keep.tile([P, P // ROT, ROT], F32)
         turns = keep.tile([P, 1], F32)
         nc.vector.scalar_tensor_tensor(
             out=turns_diag[:], in0=ident[:].rearrange("p (j c) -> p j c", c=ROT), scalar=1.0,
             in1=turns_row[:].rearrange("p f i -> p (f i)").unsqueeze(1).to_broadcast([P, P // ROT, ROT]),
             op0=ALU.mult, op1=ALU.mult, accum_out=turns[:])
+        nc.vector.tensor_copy(out=b_rows[0:PAIRS, :], in_=b_raw[:])
+        nc.vector.tensor_copy(
+            out=b_rot_rows[0:PAIRS, :].rearrange("p (r h c) -> p r h c", r=2, h=2),
+            in_=b_raw[:].rearrange("p (h r c) -> p r h c", h=2, r=3)[:, 0:2, :, 0:ROT])
         whole_sin = keep.tile([P, S], I32)
         whole_cos = keep.tile([P, S], I32)
         frac_sin = keep.tile([P, S], F32)
@@ -110,11 +114,14 @@ def tile_pgtattention_pa_kernel(tc, hidden_states, W_qkv, b_qkv, out_0, out_1, o
                                        op0=ALU.mult, op1=ALU.subtract)
         sin_t = keep.tile([P, S], F32)
         cos_t = keep.tile([P, S], F32)
-        nc.scalar.activation(out=sin_t[:], in_=frac_sin[:], func=ACT.Sin, scale=2 * math.pi)
-        nc.scalar.activation(out=cos_t[:], in_=frac_cos[:], func=ACT.Sin, scale=2 * math.pi, bias=math.pi / 2)
 
-        b_all = []
-        for pair in range(PAIRS):
+        def tables():
+            nc.scalar.activation(out=sin_t[:], in_=frac_sin[:], func=ACT.Sin, scale=2 * math.pi)
+            nc.scalar.activation(out=cos_t[:], in_=frac_cos[:], func=ACT.Sin, scale=2 * math.pi, bias=math.pi / 2)
+
+        b_all = {}
+
+        def spread_bias(pair):
             spread = bank([P, PAIR_COLS], BF16)
             for c0 in range(0, PAIR_COLS, 512):
                 cols = slice(c0, min(c0 + 512, PAIR_COLS))
@@ -122,11 +129,14 @@ def tile_pgtattention_pa_kernel(tc, hidden_states, W_qkv, b_qkv, out_0, out_1, o
                                  rhs=b_rows[:, cols], start=True, stop=True)
             b_pair = keep.tile([P, PAIR_COLS], BF16, name="b_pair_%d" % pair)
             nc.scalar.copy(out=b_pair[:], in_=spread[:])
-            b_all.append(b_pair[:].rearrange("p (h r c) -> p r h c", h=2, r=3))
-        b_rot_ps = bank([P, PAIRS], F32)
-        nc.tensor.matmul(b_rot_ps[:], lhsT=b_rot_rows[:], rhs=pick[:], start=True, stop=True)
+            b_all[pair] = b_pair[:].rearrange("p (h r c) -> p r h c", h=2, r=3)
+
         b_rot = keep.tile([P, PAIRS], F32)
-        nc.scalar.copy(out=b_rot[:], in_=b_rot_ps[:])
+
+        def turn_bias():
+            b_rot_ps = bank([P, PAIRS], F32)
+            nc.tensor.matmul(b_rot_ps[:], lhsT=b_rot_rows[:], rhs=pick[:], start=True, stop=True)
+            nc.scalar.copy(out=b_rot[:], in_=b_rot_ps[:])
 
         widths = {"rot": 4 * ROT, "rest": 4 * REST, "v": 2 * HD}
         w_side = {}
@@ -134,22 +144,28 @@ def tile_pgtattention_pa_kernel(tc, hidden_states, W_qkv, b_qkv, out_0, out_1, o
         w_scales = {}
 
         def interleave(copy, pair, g, piece):
-            side = work.tile([P, widths[piece] * PACK], BF16, name="side_" + piece, align_bytes=64)
-            w_side[pair, g, piece] = side
+            if g == 0:
+                w_side[pair, piece] = work.tile([P, PASSES, widths[piece] * PACK], BF16, name="side_" + piece, bufs=2,
+                                                align_bytes=64)
+            side = w_side[pair, piece][:, g, :]
             src = w_raw[pair, g][:].rearrange("p j (h r c) -> p r h c j", h=2, r=3)
             if piece == "rot":
-                copy(out=side[:].rearrange("p (r h c j) -> p r h c j", r=2, h=2, j=PACK), in_=src[:, 0:2, :, 0:ROT, :])
+                copy(out=side.rearrange("p (r h c j) -> p r h c j", r=2, h=2, j=PACK), in_=src[:, 0:2, :, 0:ROT, :])
                 return
             parts = [src[:, 2]] if piece == "v" else [src[:, r, :, ROT:HD, :] for r in range(2)]
-            dst = side[:].rearrange("p (r h c i j) -> p r h c j i", r=len(parts), h=2, i=4, j=PACK)
+            dst = side.rearrange("p (r h c i j) -> p r h c j i", r=len(parts), h=2, i=4, j=PACK)
             for r, part in enumerate(parts):
                 copy(out=dst[:, r], in_=part.rearrange("p h (c i) j -> p h c j i", i=4))
 
-        def quantize_w(pair, g, piece):
-            key = (pair, g, piece)
-            w_codes[key] = keep.tile([P, widths[piece]], U32, name="w_codes_%d_%d_%s" % key, align_bytes=64)
-            w_scales[key] = keep.tile([P, widths[piece]], U8, name="w_scales_%d_%d_%s" % key, align_bytes=64)
-            nc.vector.quantize_mx(out=w_codes[key][:].bitcast(E4M3), scales=w_scales[key][:], in_=w_side[key][:])
+        def quantize_piece(pair, piece):
+            key = (pair, piece)
+            w_codes[key] = keep.tile([P, PASSES, widths[piece]], U32, name="w_codes_%d_%s" % key, align_bytes=64)
+            w_scales[key] = keep.tile([P, PASSES, widths[piece]], U8, name="w_scales_%d_%s" % key, align_bytes=64)
+            spans = [slice(g, g + 1) for g in range(PASSES)] if piece == "rest" else [slice(0, PASSES)]
+            for span in spans:
+                nc.vector.quantize_mx(out=w_codes[key][:, span, :].rearrange("p g c -> p (g c)").bitcast(E4M3),
+                                      scales=w_scales[key][:, span, :].rearrange("p g c -> p (g c)"),
+                                      in_=w_side[key][:, span, :].rearrange("p g c -> p (g c)"))
 
         x_side = {}
         x_codes = {}
@@ -179,10 +195,10 @@ def tile_pgtattention_pa_kernel(tc, hidden_states, W_qkv, b_qkv, out_0, out_1, o
         def product(out, b, t, pair, piece, cols):
             toks = slice(t * P, (t + 1) * P)
             for g in range(PASSES):
-                key = (pair, g, piece)
+                key = (pair, piece)
                 nc.tensor.matmul_mx(
                     out=out, lhsT=x_codes[b, g][:, toks].bitcast(E5M2), lhsT_scale=x_scales[b, g][:, toks],
-                    rhs=w_codes[key][:, cols].bitcast(E4M3), rhs_scale=w_scales[key][:, cols],
+                    rhs=w_codes[key][:, g, cols].bitcast(E4M3), rhs_scale=w_scales[key][:, g, cols],
                     start=(g == 0), stop=(g == PASSES - 1))
 
         qk_stage = {}
@@ -215,16 +231,26 @@ def tile_pgtattention_pa_kernel(tc, hidden_states, W_qkv, b_qkv, out_0, out_1, o
 
         def rot_product(s):
             pair, b = divmod(s, B)
-            acc = psum.tile([P, S], F32, name="rot_acc")
+            acc = bank([P, S], F32)
             rot_acc[s] = acc
             for g in range(PASSES):
-                key = (pair, g, "rot")
+                key = (pair, "rot")
                 nc.tensor.matmul_mx(
-                    out=acc[:], lhsT=w_codes[key][:].bitcast(E4M3), lhsT_scale=w_scales[key][:],
+                    out=acc[:], lhsT=w_codes[key][:, g, :].bitcast(E4M3), lhsT_scale=w_scales[key][:, g, :],
                     rhs=x_codes[b, g][:].bitcast(E5M2), rhs_scale=x_scales[b, g][:],
                     start=(g == 0), stop=(g == PASSES - 1))
 
         def rot_terms(s):
+            pair = s // B
+            plain = work.tile([P, S], F32, name="plain", bufs=2)
+            nc.scalar.activation(out=plain[:], in_=rot_acc[s][:], func=ACT.Identity, bias=b_rot[:, pair:pair + 1])
+            by_cos = work.tile([P, S], F32, name="by_cos", bufs=2)
+            by_sin = work.tile([P, S], F32, name="by_sin", bufs=2)
+            terms[s] = (by_cos, by_sin)
+            for term, table in ((by_cos, cos_t), (by_sin, sin_t)):
+                nc.gpsimd.tensor_tensor(out=term[:], in0=plain[:], in1=table[:], op=ALU.mult)
+
+        def rot_terms_from_psum(s):
             pair = s // B
             by_cos = work.tile([P, S], F32, name="by_cos", bufs=2)
             by_sin = work.tile([P, S], F32, name="by_sin", bufs=2)
@@ -233,93 +259,133 @@ def tile_pgtattention_pa_kernel(tc, hidden_states, W_qkv, b_qkv, out_0, out_1, o
                 nc.vector.scalar_tensor_tensor(out=term[:], in0=rot_acc[s][:], scalar=b_rot[:, pair:pair + 1],
                                                in1=table[:], op0=ALU.add, op1=ALU.mult)
 
+        rot_turned = {}
+
         def rot_finish(s):
             by_cos, by_sin = terms[s]
-            turned = psum.tile([P, TT, P], F32, name="rot_turned")
+            turned = bank([P, TT, P], F32)
             for t in range(TT):
                 toks = slice(t * P, (t + 1) * P)
                 nc.tensor.matmul(turned[:, t, :], lhsT=by_cos[:, toks], rhs=ident[:], start=True, stop=False,
                                  is_transpose=True)
                 nc.tensor.matmul(turned[:, t, :], lhsT=by_sin[:, toks], rhs=swap[:], start=False, stop=True,
                                  is_transpose=True)
-            nc.scalar.copy(out=qk_stage[s][:, :, :, :, 0:ROT].rearrange("p r h t c -> p (r h) t c"),
-                           in_=turned[:].rearrange("p t (j c) -> p j t c", c=ROT))
+            rot_turned[s] = turned
 
-        def store(s, r):
+        def rot_out(s):
+            nc.vector.tensor_copy(out=qk_stage[s][:, :, :, :, 0:ROT].rearrange("p r h t c -> p (r h) t c"),
+                                  in_=rot_turned[s][:].rearrange("p t (j c) -> p j t c", c=ROT))
+
+        def store(s, r, tiles=slice(0, TT)):
             pair, b = divmod(s, B)
             src = v_stage[s][:] if r == 2 else qk_stage[s][:, r]
-            dst = outs[r][b, 2 * pair:2 * pair + 2].rearrange("h (m t) c -> m h (t c)", t=TT)
-            nc.sync.dma_start(out=dst, in_=src.rearrange("p h t c -> p h (t c)"))
+            dst = outs[r][b, 2 * pair:2 * pair + 2].rearrange("h (m t) c -> m h t c", t=TT)
+            nc.sync.dma_start(out=dst[:, :, tiles, :].rearrange("m h t c -> m h (t c)"),
+                              in_=src[:, :, tiles, :].rearrange("p h t c -> p h (t c)"))
 
+        def interleave_pieces(pair, pieces):
+            for piece in pieces:
+                for g in range(PASSES):
+                    interleave(nc.scalar.copy, pair, g, piece)
+
+
+        tables()
+        for pair in range(PAIRS):
+            spread_bias(pair)
+        turn_bias()
         for g in range(PASSES):
             interleave(nc.vector.tensor_copy, 0, g, "rest")
-            interleave(nc.vector.tensor_copy, 0, g, "rot")
-        for piece in ("rest", "rot"):
-            for g in range(PASSES):
-                quantize_w(0, g, piece)
+        quantize_piece(0, "rest")
         for t in range(TT):
             transpose_x(0, t)
-        for g in range(PASSES):
-            interleave(nc.scalar.copy, 0, g, "v")
         open_step(0)
+        open_step(1)
+        for g in range(PASSES):
+            interleave(nc.vector.tensor_copy, 0, g, "rot")
         quantize_x(0, 0)
         quantize_x(0, 1)
+        interleave(nc.scalar.copy, 0, 0, "v")
         rest_tile(0, 0)
+        transpose_x(1, 0)
+        transpose_x(1, 1)
+        quantize_piece(0, "rot")
         quantize_x(0, 2)
         quantize_x(0, 3)
         rest_tile(0, 1)
-        rot_product(0)
         rest_tile(0, 2)
-        for g in range(PASSES):
-            quantize_w(0, g, "v")
-        rot_terms(0)
+        quantize_x(1, 0)
         rest_tile(0, 3)
-        for t in range(TT):
-            transpose_x(1, t)
+        rot_product(0)
+        interleave(nc.scalar.copy, 0, 1, "v")
+        transpose_x(1, 2)
+        transpose_x(1, 3)
+        quantize_x(1, 1)
+        rot_terms_from_psum(0)
+        quantize_piece(0, "v")
+        quantize_x(1, 2)
+        quantize_x(1, 3)
+        interleave_pieces(1, ("rot", "v", "rest"))
         v_tiles(0, 0)
-        rot_finish(0)
-        store(0, 0)
-        store(0, 1)
+        rot_product(1)
         v_tiles(0, 2)
         store(0, 2)
-        for t in range(TT):
-            quantize_x(1, t)
-        rot_product(1)
-        for piece in ("rot", "rest"):
-            for g in range(PASSES):
-                interleave(nc.scalar.copy, 1, g, piece)
+        rot_finish(0)
+        rot_terms_from_psum(1)
+        v_tiles(1, 0)
+        rot_out(0)
+        store(0, 0)
+        store(0, 1)
+        v_tiles(1, 2)
+        store(1, 2)
+        rot_finish(1)
+        rot_out(1)
 
-        for s in range(1, STEPS):
-            pair, b = divmod(s, B)
+        for pair in range(1, PAIRS):
+            first, second = B * pair, B * pair + 1
             more = pair + 1 < PAIRS
-            open_step(s)
+            for piece in ("rot", "v", "rest"):
+                quantize_piece(pair, piece)
+            for t0 in range(0, TT, 2):
+                rest_tile(first - 1, t0)
+                rest_tile(first - 1, t0 + 1)
+                store(first - 1, 0, slice(t0, t0 + 2))
+                store(first - 1, 1, slice(t0, t0 + 2))
+                rot_product(first + t0 // 2)
+                rot_terms(first + t0 // 2)
+                if more and t0 == 0:
+                    interleave_pieces(pair + 1, ("rot",))
+            open_step(first)
+            open_step(second)
+            v_tiles(first, 0)
+            v_tiles(first, 2)
+            store(first, 2)
+            if not more:
+                break
+            interleave_pieces(pair + 1, ("v", "rest"))
+            for t in range(TT):
+                rest_tile(first, t)
+            v_tiles(second, 0)
+            v_tiles(second, 2)
+            rot_finish(first)
+            rot_finish(second)
+            rot_out(first)
+            store(first, 0)
+            store(first, 1)
+            store(second, 2)
+            rot_out(second)
+
+        first, second = STEPS - 2, STEPS - 1
+        v_tiles(second, 0)
+        v_tiles(second, 2)
+        store(second, 2)
+        for s in (first, second):
             rest_tile(s, 0)
-            if s == 1:
-                rot_terms(1)
-            rest_tile(s, 1)
             rot_finish(s)
-            if more and b == 0:
-                for piece in ("rot", "rest"):
-                    for g in range(PASSES):
-                        interleave(nc.scalar.copy, pair + 1, g, piece)
-            if more and b == 1:
-                for g in range(PASSES):
-                    interleave(nc.scalar.copy, pair + 1, g, "v")
-            for g in range(PASSES):
-                if b == 0:
-                    quantize_w(pair, g, "v")
-                elif more:
-                    quantize_w(pair + 1, g, "rot")
+            rest_tile(s, 1)
+            rot_out(s)
+            store(s, 0, slice(0, 2))
+            store(s, 1, slice(0, 2))
             rest_tile(s, 2)
             rest_tile(s, 3)
-            store(s, 0)
-            store(s, 1)
-            if s + 1 < STEPS:
-                rot_product(s + 1)
-                if b == 1:
-                    for g in range(PASSES):
-                        quantize_w(pair + 1, g, "rest")
-                rot_terms(s + 1)
-            v_tiles(s, 0)
-            v_tiles(s, 2)
-            store(s, 2)
+            store(s, 0, slice(2, 4))
+            store(s, 1, slice(2, 4))

@@ -112,12 +112,13 @@ def tile_pgtattention_pa_kernel(tc, hidden_states, W_qkv, b_qkv, out_0, out_1, o
                                        op0=ALU.mult, op1=ALU.subtract)
         nc.vector.scalar_tensor_tensor(out=frac_cos[:], in0=pos[:], scalar=turns[:], in1=whole_cos[:],
                                        op0=ALU.mult, op1=ALU.subtract)
-        sin_t = keep.tile([P, S], F32)
-        cos_t = keep.tile([P, S], F32)
+        trig = keep.tile([P, 2, S], F32)
+        cos_t = trig[:, 0, :]
+        sin_t = trig[:, 1, :]
 
         def tables():
-            nc.scalar.activation(out=sin_t[:], in_=frac_sin[:], func=ACT.Sin, scale=2 * math.pi)
-            nc.scalar.activation(out=cos_t[:], in_=frac_cos[:], func=ACT.Sin, scale=2 * math.pi, bias=math.pi / 2)
+            nc.scalar.activation(out=sin_t, in_=frac_sin[:], func=ACT.Sin, scale=2 * math.pi)
+            nc.scalar.activation(out=cos_t, in_=frac_cos[:], func=ACT.Sin, scale=2 * math.pi, bias=math.pi / 2)
 
         b_all = {}
 
@@ -244,20 +245,18 @@ def tile_pgtattention_pa_kernel(tc, hidden_states, W_qkv, b_qkv, out_0, out_1, o
             pair = s // B
             plain = work.tile([P, S], F32, name="plain", bufs=2)
             nc.scalar.activation(out=plain[:], in_=rot_acc[s][:], func=ACT.Identity, bias=b_rot[:, pair:pair + 1])
-            by_cos = work.tile([P, S], F32, name="by_cos", bufs=2)
-            by_sin = work.tile([P, S], F32, name="by_sin", bufs=2)
-            terms[s] = (by_cos, by_sin)
-            for term, table in ((by_cos, cos_t), (by_sin, sin_t)):
-                nc.gpsimd.tensor_tensor(out=term[:], in0=plain[:], in1=table[:], op=ALU.mult)
+            both = work.tile([P, 2, S], F32, name="both", bufs=2)
+            terms[s] = (both[:, 0, :], both[:, 1, :])
+            nc.gpsimd.tensor_tensor(out=both[:], in0=plain[:].unsqueeze(1).to_broadcast([P, 2, S]), in1=trig[:],
+                                    op=ALU.mult)
 
         def rot_terms_from_psum(s):
             pair = s // B
-            by_cos = work.tile([P, S], F32, name="by_cos", bufs=2)
-            by_sin = work.tile([P, S], F32, name="by_sin", bufs=2)
-            terms[s] = (by_cos, by_sin)
-            for term, table in ((by_cos, cos_t), (by_sin, sin_t)):
-                nc.vector.scalar_tensor_tensor(out=term[:], in0=rot_acc[s][:], scalar=b_rot[:, pair:pair + 1],
-                                               in1=table[:], op0=ALU.add, op1=ALU.mult)
+            both = work.tile([P, 2, S], F32, name="both", bufs=2)
+            terms[s] = (both[:, 0, :], both[:, 1, :])
+            for term, table in zip(terms[s], (cos_t, sin_t)):
+                nc.vector.scalar_tensor_tensor(out=term, in0=rot_acc[s][:], scalar=b_rot[:, pair:pair + 1],
+                                               in1=table, op0=ALU.add, op1=ALU.mult)
 
         rot_turned = {}
 
@@ -324,7 +323,7 @@ def tile_pgtattention_pa_kernel(tc, hidden_states, W_qkv, b_qkv, out_0, out_1, o
         quantize_piece(0, "v")
         quantize_x(1, 2)
         quantize_x(1, 3)
-        interleave_pieces(1, ("rot", "v", "rest"))
+        interleave_pieces(1, ("rest", "v", "rot"))
         v_tiles(0, 0)
         rot_product(1)
         v_tiles(0, 2)
@@ -337,42 +336,45 @@ def tile_pgtattention_pa_kernel(tc, hidden_states, W_qkv, b_qkv, out_0, out_1, o
         store(0, 1)
         v_tiles(1, 2)
         store(1, 2)
-        rot_finish(1)
-        rot_out(1)
 
         for pair in range(1, PAIRS):
             first, second = B * pair, B * pair + 1
             more = pair + 1 < PAIRS
-            for piece in ("rot", "v", "rest"):
+            for piece in ("rest", "v", "rot"):
                 quantize_piece(pair, piece)
+            if more:
+                interleave(nc.scalar.copy, pair + 1, 0, "rest")
+            rot_finish(first - 1)
+            rot_out(first - 1)
             for t0 in range(0, TT, 2):
                 rest_tile(first - 1, t0)
                 rest_tile(first - 1, t0 + 1)
                 store(first - 1, 0, slice(t0, t0 + 2))
                 store(first - 1, 1, slice(t0, t0 + 2))
-                rot_product(first + t0 // 2)
-                rot_terms(first + t0 // 2)
-                if more and t0 == 0:
-                    interleave_pieces(pair + 1, ("rot",))
+            rot_product(first)
+            rot_terms(first)
+            if more:
+                interleave_pieces(pair + 1, ("rot",))
             open_step(first)
             open_step(second)
             v_tiles(first, 0)
+            rot_product(second)
+            rot_terms(second)
             v_tiles(first, 2)
             store(first, 2)
             if not more:
                 break
-            interleave_pieces(pair + 1, ("v", "rest"))
+            interleave(nc.scalar.copy, pair + 1, 1, "rest")
+            interleave_pieces(pair + 1, ("v",))
             for t in range(TT):
                 rest_tile(first, t)
             v_tiles(second, 0)
             v_tiles(second, 2)
             rot_finish(first)
-            rot_finish(second)
             rot_out(first)
             store(first, 0)
             store(first, 1)
             store(second, 2)
-            rot_out(second)
 
         first, second = STEPS - 2, STEPS - 1
         v_tiles(second, 0)
@@ -380,8 +382,8 @@ def tile_pgtattention_pa_kernel(tc, hidden_states, W_qkv, b_qkv, out_0, out_1, o
         store(second, 2)
         for s in (first, second):
             rest_tile(s, 0)
-            rot_finish(s)
             rest_tile(s, 1)
+            rot_finish(s)
             rot_out(s)
             store(s, 0, slice(0, 2))
             store(s, 1, slice(0, 2))

@@ -47,25 +47,29 @@ def tile_pgtattention_pa_kernel(tc, hidden_states, W_qkv, b_qkv, out_0, out_1, o
         w_raw = {}
         x_raw = {}
 
-        def load_w(pair, passes=range(PASSES)):
-            for g in passes:
-                w_raw[pair, g] = keep.tile([P, PACK, PAIR_COLS], BF16, name="w_raw_%d_%d" % (pair, g))
-                rows = W_qkv[g * P * PACK:(g + 1) * P * PACK, pair * PAIR_COLS:(pair + 1) * PAIR_COLS]
-                nc.sync.dma_start(out=w_raw[pair, g][:], in_=rows.rearrange("(p j) c -> p j c", j=PACK))
+        def load_w(pair0, count):
+            for g in range(PASSES):
+                raw = keep.tile([P, PACK, count * PAIR_COLS], BF16, name="w_raw_%d_%d" % (pair0, g))
+                rows = W_qkv[g * P * PACK:(g + 1) * P * PACK, pair0 * PAIR_COLS:(pair0 + count) * PAIR_COLS]
+                nc.sync.dma_start(out=raw[:], in_=rows.rearrange("(p j) c -> p j c", j=PACK))
+                for i in range(count):
+                    w_raw[pair0 + i, g] = raw[:, :, i * PAIR_COLS:(i + 1) * PAIR_COLS]
 
         x_rows = [hidden_states[b].rearrange("(m t) k -> m t k", t=TT) for b in range(B)]
 
-        def load_x(b, t):
-            tile_x = keep.tile([P, H], BF16, name="x_raw_%d_%d" % (b, t))
-            nc.sync.dma_start(out=tile_x[:], in_=x_rows[b][:, t, :])
-            x_raw[b, t] = tile_x[:]
+        def load_x(b, t0, count):
+            raw = keep.tile([P, count, H], BF16, name="x_raw_%d_%d" % (b, t0))
+            nc.sync.dma_start(out=raw[:], in_=x_rows[b][:, t0:t0 + count, :])
+            for i in range(count):
+                x_raw[b, t0 + i] = raw[:, i, :]
 
-        load_w(0)
+        load_w(0, 1)
         for b in range(B):
             for t in range(TT):
-                load_x(b, t)
-        for pair in range(1, PAIRS):
-            load_w(pair)
+                load_x(b, t, 1)
+        load_w(1, 1)
+        load_w(2, 1)
+        load_w(3, 1)
 
 
         ident = keep.tile([P, P], F32)
@@ -149,7 +153,7 @@ def tile_pgtattention_pa_kernel(tc, hidden_states, W_qkv, b_qkv, out_0, out_1, o
                 w_side[pair, piece] = work.tile([P, PASSES, widths[piece] * PACK], BF16, name="side_" + piece, bufs=2,
                                                 align_bytes=64)
             side = w_side[pair, piece][:, g, :]
-            src = w_raw[pair, g][:].rearrange("p j (h r c) -> p r h c j", h=2, r=3)
+            src = w_raw[pair, g].rearrange("p j (h r c) -> p r h c j", h=2, r=3)
             if piece == "rot":
                 copy(out=side.rearrange("p (r h c j) -> p r h c j", r=2, h=2, j=PACK), in_=src[:, 0:2, :, 0:ROT, :])
                 return
@@ -271,15 +275,15 @@ def tile_pgtattention_pa_kernel(tc, hidden_states, W_qkv, b_qkv, out_0, out_1, o
                                  is_transpose=True)
             rot_turned[s] = turned
 
-        def rot_out(s):
-            nc.vector.tensor_copy(out=qk_stage[s][:, :, :, :, 0:ROT].rearrange("p r h t c -> p (r h) t c"),
-                                  in_=rot_turned[s][:].rearrange("p t (j c) -> p j t c", c=ROT))
+        def rot_out(s, copy=nc.scalar.copy):
+            copy(out=qk_stage[s][:, :, :, :, 0:ROT].rearrange("p r h t c -> p (r h) t c"),
+                 in_=rot_turned[s][:].rearrange("p t (j c) -> p j t c", c=ROT))
 
-        def store(s, r, tiles=slice(0, TT)):
+        def store(s, r, tiles=slice(0, TT), queue=nc.sync):
             pair, b = divmod(s, B)
             src = v_stage[s][:] if r == 2 else qk_stage[s][:, r]
             dst = outs[r][b, 2 * pair:2 * pair + 2].rearrange("h (m t) c -> m h t c", t=TT)
-            nc.sync.dma_start(out=dst[:, :, tiles, :].rearrange("m h t c -> m h (t c)"),
+            queue.dma_start(out=dst[:, :, tiles, :].rearrange("m h t c -> m h (t c)"),
                               in_=src[:, :, tiles, :].rearrange("p h t c -> p h (t c)"))
 
         def interleave_pieces(pair, pieces):
@@ -319,11 +323,11 @@ def tile_pgtattention_pa_kernel(tc, hidden_states, W_qkv, b_qkv, out_0, out_1, o
         transpose_x(1, 2)
         transpose_x(1, 3)
         quantize_x(1, 1)
-        rot_terms_from_psum(0)
         quantize_piece(0, "v")
+        rot_terms_from_psum(0)
         quantize_x(1, 2)
         quantize_x(1, 3)
-        interleave_pieces(1, ("rest", "v", "rot"))
+        interleave_pieces(1, ("rest", "rot", "v"))
         v_tiles(0, 0)
         rot_product(1)
         v_tiles(0, 2)
@@ -331,7 +335,7 @@ def tile_pgtattention_pa_kernel(tc, hidden_states, W_qkv, b_qkv, out_0, out_1, o
         rot_finish(0)
         rot_terms_from_psum(1)
         v_tiles(1, 0)
-        rot_out(0)
+        rot_out(0, nc.vector.tensor_copy)
         store(0, 0)
         store(0, 1)
         v_tiles(1, 2)
@@ -340,10 +344,11 @@ def tile_pgtattention_pa_kernel(tc, hidden_states, W_qkv, b_qkv, out_0, out_1, o
         for pair in range(1, PAIRS):
             first, second = B * pair, B * pair + 1
             more = pair + 1 < PAIRS
-            for piece in ("rest", "v", "rot"):
+            for piece in ("rest", "rot", "v"):
                 quantize_piece(pair, piece)
             if more:
-                interleave(nc.scalar.copy, pair + 1, 0, "rest")
+                for g in range(PASSES):
+                    interleave(nc.vector.tensor_copy, pair + 1, g, "rot")
             rot_finish(first - 1)
             rot_out(first - 1)
             for t0 in range(0, TT, 2):
@@ -351,10 +356,11 @@ def tile_pgtattention_pa_kernel(tc, hidden_states, W_qkv, b_qkv, out_0, out_1, o
                 rest_tile(first - 1, t0 + 1)
                 store(first - 1, 0, slice(t0, t0 + 2))
                 store(first - 1, 1, slice(t0, t0 + 2))
-            rot_product(first)
-            rot_terms(first)
+                if t0 == 0:
+                    rot_product(first)
+                    rot_terms(first)
             if more:
-                interleave_pieces(pair + 1, ("rot",))
+                interleave(nc.scalar.copy, pair + 1, 0, "rest")
             open_step(first)
             open_step(second)
             v_tiles(first, 0)
@@ -365,13 +371,13 @@ def tile_pgtattention_pa_kernel(tc, hidden_states, W_qkv, b_qkv, out_0, out_1, o
             if not more:
                 break
             interleave(nc.scalar.copy, pair + 1, 1, "rest")
-            interleave_pieces(pair + 1, ("v",))
             for t in range(TT):
                 rest_tile(first, t)
-            v_tiles(second, 0)
-            v_tiles(second, 2)
             rot_finish(first)
             rot_out(first)
+            interleave_pieces(pair + 1, ("v",))
+            v_tiles(second, 0)
+            v_tiles(second, 2)
             store(first, 0)
             store(first, 1)
             store(second, 2)
@@ -380,14 +386,23 @@ def tile_pgtattention_pa_kernel(tc, hidden_states, W_qkv, b_qkv, out_0, out_1, o
         v_tiles(second, 0)
         v_tiles(second, 2)
         store(second, 2)
-        for s in (first, second):
-            rest_tile(s, 0)
-            rest_tile(s, 1)
-            rot_finish(s)
-            rot_out(s)
-            store(s, 0, slice(0, 2))
-            store(s, 1, slice(0, 2))
-            rest_tile(s, 2)
-            rest_tile(s, 3)
-            store(s, 0, slice(2, 4))
-            store(s, 1, slice(2, 4))
+        rest_tile(first, 0)
+        rest_tile(first, 1)
+        rot_finish(first)
+        rot_out(first)
+        store(first, 0, slice(0, 2))
+        store(first, 1, slice(0, 2), nc.scalar)
+        rest_tile(first, 2)
+        rest_tile(first, 3)
+        store(first, 0, slice(2, 4))
+        store(first, 1, slice(2, 4), nc.scalar)
+        rot_finish(second)
+        rot_out(second)
+        rest_tile(second, 0)
+        rest_tile(second, 1)
+        store(second, 0, slice(0, 2))
+        store(second, 1, slice(0, 2), nc.scalar)
+        rest_tile(second, 2)
+        rest_tile(second, 3)
+        store(second, 0, slice(2, 4))
+        store(second, 1, slice(2, 4), nc.scalar)

@@ -24,9 +24,15 @@ PASSES = H // (P * PACK)
 TT = S // P
 PAIRS = NH // 2
 PAIR_COLS = 2 * 3 * HD
+STEPS = PAIRS * B
 HALF = ROT // 2
 REST = HD - ROT
-STEPS = PAIRS * B
+WIDTH = {"rot": 4 * ROT, "rest": 4 * REST, "v": 2 * HD}
+REST_SPLIT = 256
+RUN = 4
+PSUM_BANKS = 8
+STAGE_BUFS = 5
+Q, K, V = 0, 1, 2
 
 
 def tile_pgtattention_pa_kernel(tc, hidden_states, W_qkv, b_qkv, out_0, out_1, out_2):
@@ -35,15 +41,16 @@ def tile_pgtattention_pa_kernel(tc, hidden_states, W_qkv, b_qkv, out_0, out_1, o
 
     with ExitStack() as ctx:
         keep = ctx.enter_context(tc.tile_pool(name="keep", bufs=1))
-        work = ctx.enter_context(tc.tile_pool(name="work", bufs=3))
-        psum = ctx.enter_context(tc.psum_pool(name="psum", bufs=1))
+        work = ctx.enter_context(tc.tile_pool(name="work", bufs=2))
+        psum = ctx.enter_context(tc.psum_pool(name="psum", bufs=PSUM_BANKS))
         ctx.enter_context(tc.manual_schedule())
 
         def bank(shape, dtype):
-            return psum.tile(shape, dtype, name="bank", tag="bank", bufs=8)
+            return psum.tile(shape, dtype, name="bank", tag="bank")
 
         b_raw = keep.tile([PAIRS, PAIR_COLS], BF16)
         nc.sync.dma_start(out=b_raw[:], in_=b_qkv.rearrange("(r c) -> r c", r=PAIRS))
+
         w_raw = {}
         x_raw = {}
 
@@ -55,22 +62,14 @@ def tile_pgtattention_pa_kernel(tc, hidden_states, W_qkv, b_qkv, out_0, out_1, o
                 for i in range(count):
                     w_raw[pair0 + i, g] = raw[:, :, i * PAIR_COLS:(i + 1) * PAIR_COLS]
 
-        x_rows = [hidden_states[b].rearrange("(m t) k -> m t k", t=TT) for b in range(B)]
-
-        def load_x(b, t0, count):
-            raw = keep.tile([P, count, H], BF16, name="x_raw_%d_%d" % (b, t0))
-            nc.sync.dma_start(out=raw[:], in_=x_rows[b][:, t0:t0 + count, :])
-            for i in range(count):
-                x_raw[b, t0 + i] = raw[:, i, :]
-
         load_w(0, 1)
         for b in range(B):
             for t in range(TT):
-                load_x(b, t, 1)
+                raw_x = keep.tile([P, H], BF16, name="x_raw_%d_%d" % (b, t))
+                nc.sync.dma_start(out=raw_x[:], in_=hidden_states[b].rearrange("(m t) k -> m t k", t=TT)[:, t, :])
+                x_raw[b, t] = raw_x
         load_w(1, 1)
-        load_w(2, 1)
-        load_w(3, 1)
-
+        load_w(2, PAIRS - 2)
 
         ident = keep.tile([P, P], F32)
         make_identity(nc, ident[:])
@@ -80,92 +79,90 @@ def tile_pgtattention_pa_kernel(tc, hidden_states, W_qkv, b_qkv, out_0, out_1, o
         pick = keep.tile([P, PAIRS], BF16)
         nc.scalar.copy(out=pick[:], in_=ident[:, 0:PAIRS])
         swap = keep.tile([P, P], F32)
-        ident_h = ident[:].rearrange("p (j f i) -> p j f i", f=2, i=HALF)
-        swap_h = swap[:].rearrange("p (j f i) -> p j f i", f=2, i=HALF)
+        ident_halves = ident[:].rearrange("p (n f i) -> p n f i", f=2, i=HALF)
+        swap_halves = swap[:].rearrange("p (n f i) -> p n f i", f=2, i=HALF)
         for f in range(2):
-            nc.scalar.copy(out=swap_h[:, :, f, :], in_=ident_h[:, :, 1 - f, :])
+            nc.scalar.copy(out=swap_halves[:, :, f, :], in_=ident_halves[:, :, 1 - f, :])
+
+        plain_cols = WIDTH["rest"] + WIDTH["v"]
         b_rows = keep.tile([P, PAIR_COLS], BF16)
-        b_rot_rows = keep.tile([P, P], BF16)
         nc.vector.memset(b_rows[:], 0.0)
-        nc.vector.memset(b_rot_rows[:], 0.0)
 
         one = keep.tile([P, 1], F32)
         nc.vector.memset(one[:], 1.0)
         turns_row = keep.tile([P, 2, HALF], F32)
         for i in range(HALF):
-            nc.vector.tensor_scalar(out=turns_row[:, 0, i:i + 1], in0=one[:], scalar1=BASE ** (-i / HALF) / (2 * math.pi),
-                                    scalar2=None, op0=ALU.mult)
-        nc.vector.tensor_scalar(out=turns_row[:, 1, :], in0=turns_row[:, 0, :], scalar1=-1.0, scalar2=None, op0=ALU.mult)
+            nc.vector.tensor_scalar(out=turns_row[:, 0, i:i + 1], in0=one[:],
+                                    scalar1=BASE ** (-i / HALF) / (2 * math.pi), scalar2=None, op0=ALU.mult)
+        nc.vector.tensor_scalar(out=turns_row[:, 1, :], in0=turns_row[:, 0, :], scalar1=-1.0, scalar2=None,
+                                op0=ALU.mult)
         turns_diag = keep.tile([P, P // ROT, ROT], F32)
+        nc.vector.tensor_tensor(
+            out=turns_diag[:], in0=ident[:].rearrange("p (n c) -> p n c", c=ROT),
+            in1=turns_row[:].rearrange("p f i -> p (f i)").unsqueeze(1).to_broadcast([P, P // ROT, ROT]), op=ALU.mult)
+        b_parts = b_raw[:].rearrange("p (h r c) -> p r h c", h=2, r=3)
+        nc.vector.tensor_copy(out=b_rows[0:PAIRS, 0:WIDTH["rest"]].rearrange("p (r h c) -> p r h c", r=2, h=2),
+                              in_=b_parts[:, Q:V, :, ROT:HD])
         turns = keep.tile([P, 1], F32)
-        nc.vector.scalar_tensor_tensor(
-            out=turns_diag[:], in0=ident[:].rearrange("p (j c) -> p j c", c=ROT), scalar=1.0,
-            in1=turns_row[:].rearrange("p f i -> p (f i)").unsqueeze(1).to_broadcast([P, P // ROT, ROT]),
-            op0=ALU.mult, op1=ALU.mult, accum_out=turns[:])
-        nc.vector.tensor_copy(out=b_rows[0:PAIRS, :], in_=b_raw[:])
-        nc.vector.tensor_copy(
-            out=b_rot_rows[0:PAIRS, :].rearrange("p (r h c) -> p r h c", r=2, h=2),
-            in_=b_raw[:].rearrange("p (h r c) -> p r h c", h=2, r=3)[:, 0:2, :, 0:ROT])
+        nc.vector.tensor_reduce(out=turns[:], in_=turns_diag[:].rearrange("p n c -> p (n c)"),
+                                axis=mybir.AxisListType.X, op=ALU.add)
+        nc.vector.tensor_copy(out=b_rows[0:PAIRS, WIDTH["rest"]:plain_cols].rearrange("p (h c) -> p h c", h=2),
+                              in_=b_parts[:, V])
+        nc.vector.tensor_copy(out=b_rows[0:PAIRS, plain_cols:PAIR_COLS].rearrange("p (r h c) -> p r h c", r=2, h=2),
+                              in_=b_parts[:, Q:V, :, 0:ROT])
+
         whole_sin = keep.tile([P, S], I32)
         whole_cos = keep.tile([P, S], I32)
         frac_sin = keep.tile([P, S], F32)
         frac_cos = keep.tile([P, S], F32)
         nc.vector.tensor_scalar(out=whole_sin[:], in0=pos[:], scalar1=turns[:], scalar2=None, op0=ALU.mult)
-        nc.vector.tensor_scalar(out=whole_cos[:], in0=pos[:], scalar1=turns[:], scalar2=0.25, op0=ALU.mult, op1=ALU.add)
-        nc.vector.scalar_tensor_tensor(out=frac_sin[:], in0=pos[:], scalar=turns[:], in1=whole_sin[:],
-                                       op0=ALU.mult, op1=ALU.subtract)
-        nc.vector.scalar_tensor_tensor(out=frac_cos[:], in0=pos[:], scalar=turns[:], in1=whole_cos[:],
-                                       op0=ALU.mult, op1=ALU.subtract)
+        nc.vector.tensor_scalar(out=whole_cos[:], in0=pos[:], scalar1=turns[:], scalar2=0.25,
+                                op0=ALU.mult, op1=ALU.add)
+        for frac, whole in ((frac_sin, whole_sin), (frac_cos, whole_cos)):
+            nc.vector.scalar_tensor_tensor(out=frac[:], in0=pos[:], scalar=turns[:], in1=whole[:],
+                                           op0=ALU.mult, op1=ALU.subtract)
         trig = keep.tile([P, 2, S], F32)
-        cos_t = trig[:, 0, :]
-        sin_t = trig[:, 1, :]
+        nc.scalar.activation(out=trig[:, 1, :], in_=frac_sin[:], func=ACT.Sin, scale=2 * math.pi)
+        nc.scalar.activation(out=trig[:, 0, :], in_=frac_cos[:], func=ACT.Sin, scale=2 * math.pi, bias=math.pi / 2)
 
-        def tables():
-            nc.scalar.activation(out=sin_t, in_=frac_sin[:], func=ACT.Sin, scale=2 * math.pi)
-            nc.scalar.activation(out=cos_t, in_=frac_cos[:], func=ACT.Sin, scale=2 * math.pi, bias=math.pi / 2)
-
-        b_all = {}
-
-        def spread_bias(pair):
-            spread = bank([P, PAIR_COLS], BF16)
-            for c0 in range(0, PAIR_COLS, 512):
-                cols = slice(c0, min(c0 + 512, PAIR_COLS))
+        b_plain = []
+        for pair in range(PAIRS):
+            spread = bank([P, plain_cols], BF16)
+            for cols in (slice(0, WIDTH["rest"]), slice(WIDTH["rest"], plain_cols)):
                 nc.tensor.matmul(spread[:, cols], lhsT=pick[:, pair:pair + 1].to_broadcast([P, P]),
                                  rhs=b_rows[:, cols], start=True, stop=True)
-            b_pair = keep.tile([P, PAIR_COLS], BF16, name="b_pair_%d" % pair)
+            b_pair = keep.tile([P, plain_cols], BF16, name="b_plain_%d" % pair)
             nc.scalar.copy(out=b_pair[:], in_=spread[:])
-            b_all[pair] = b_pair[:].rearrange("p (h r c) -> p r h c", h=2, r=3)
-
+            b_plain.append(b_pair)
+        b_rot_psum = bank([P, PAIRS], F32)
+        nc.tensor.matmul(b_rot_psum[:], lhsT=b_rows[:, plain_cols:PAIR_COLS], rhs=pick[:], start=True, stop=True)
         b_rot = keep.tile([P, PAIRS], F32)
+        nc.scalar.copy(out=b_rot[:], in_=b_rot_psum[:])
 
-        def turn_bias():
-            b_rot_ps = bank([P, PAIRS], F32)
-            nc.tensor.matmul(b_rot_ps[:], lhsT=b_rot_rows[:], rhs=pick[:], start=True, stop=True)
-            nc.scalar.copy(out=b_rot[:], in_=b_rot_ps[:])
-
-        widths = {"rot": 4 * ROT, "rest": 4 * REST, "v": 2 * HD}
         w_side = {}
         w_codes = {}
         w_scales = {}
 
-        def interleave(copy, pair, g, piece):
-            if g == 0:
-                w_side[pair, piece] = work.tile([P, PASSES, widths[piece] * PACK], BF16, name="side_" + piece, bufs=2,
-                                                align_bytes=64)
-            side = w_side[pair, piece][:, g, :]
-            src = w_raw[pair, g].rearrange("p j (h r c) -> p r h c j", h=2, r=3)
-            if piece == "rot":
-                copy(out=side.rearrange("p (r h c j) -> p r h c j", r=2, h=2, j=PACK), in_=src[:, 0:2, :, 0:ROT, :])
-                return
-            parts = [src[:, 2]] if piece == "v" else [src[:, r, :, ROT:HD, :] for r in range(2)]
-            dst = side.rearrange("p (r h c i j) -> p r h c j i", r=len(parts), h=2, i=4, j=PACK)
-            for r, part in enumerate(parts):
-                copy(out=dst[:, r], in_=part.rearrange("p h (c i) j -> p h c j i", i=4))
+        def interleave(copy, pair, piece, passes=range(PASSES)):
+            for g in passes:
+                if g == 0:
+                    w_side[pair, piece] = work.tile([P, PASSES, WIDTH[piece] * PACK], BF16, name="side_" + piece,
+                                                    align_bytes=64)
+                side = w_side[pair, piece][:, g, :]
+                src = w_raw[pair, g].rearrange("p j (h r c) -> p r h c j", h=2, r=3)
+                if piece == "rot":
+                    copy(out=side.rearrange("p (r h c j) -> p r h c j", r=2, h=2, j=PACK),
+                         in_=src[:, Q:V, :, 0:ROT, :])
+                else:
+                    parts = [src[:, V]] if piece == "v" else [src[:, r, :, ROT:HD, :] for r in (Q, K)]
+                    dst = side.rearrange("p (r h c i j) -> p r h c j i", r=len(parts), h=2, i=RUN, j=PACK)
+                    for r, part in enumerate(parts):
+                        copy(out=dst[:, r], in_=part.rearrange("p h (c i) j -> p h c j i", i=RUN))
 
-        def quantize_piece(pair, piece):
+        def quantize_w(pair, piece):
             key = (pair, piece)
-            w_codes[key] = keep.tile([P, PASSES, widths[piece]], U32, name="w_codes_%d_%s" % key, align_bytes=64)
-            w_scales[key] = keep.tile([P, PASSES, widths[piece]], U8, name="w_scales_%d_%s" % key, align_bytes=64)
+            w_codes[key] = keep.tile([P, PASSES, WIDTH[piece]], U32, name="w_codes_%d_%s" % key, align_bytes=64)
+            w_scales[key] = keep.tile([P, PASSES, WIDTH[piece]], U8, name="w_scales_%d_%s" % key, align_bytes=64)
             spans = [slice(g, g + 1) for g in range(PASSES)] if piece == "rest" else [slice(0, PASSES)]
             for span in spans:
                 nc.vector.quantize_mx(out=w_codes[key][:, span, :].rearrange("p g c -> p (g c)").bitcast(E4M3),
@@ -181,137 +178,114 @@ def tile_pgtattention_pa_kernel(tc, hidden_states, W_qkv, b_qkv, out_0, out_1, o
                 x_scales[b, g] = keep.tile([P, S], U8, name="x_scales_%d_%d" % (b, g), align_bytes=64)
 
         def transpose_x(b, t):
-            words = x_raw[b, t].bitcast(F32)
+            words = x_raw[b, t][:].bitcast(F32)
             turned = bank([P, PASSES, 2, P], F32)
             for g in range(PASSES):
                 for u in range(2):
                     nc.tensor.transpose(turned[:, g, u, :], words[:, 2 * P * g + u:2 * P * (g + 1):2], ident[:])
-            side = work.tile([P, PASSES, P * PACK], BF16, name="side_x", bufs=4, align_bytes=64)
-            x_side[b, t] = side
-            nc.scalar.copy(out=side[:].bitcast(F32).rearrange("p g (m u) -> p g m u", u=2),
+            x_side[b, t] = work.tile([P, PASSES, P * PACK], BF16, name="side_x", bufs=TT, align_bytes=64)
+            nc.scalar.copy(out=x_side[b, t][:].bitcast(F32).rearrange("p g (m u) -> p g m u", u=2),
                            in_=turned[:].rearrange("p g u m -> p g m u"))
 
         def quantize_x(b, t):
-            cols = slice(t * P, (t + 1) * P)
-            for g in range(PASSES):
-                nc.vector.quantize_mx(out=x_codes[b, g][:, cols].bitcast(E5M2), scales=x_scales[b, g][:, cols],
-                                      in_=x_side[b, t][:, g, :])
-
-        def product(out, b, t, pair, piece, cols):
             toks = slice(t * P, (t + 1) * P)
             for g in range(PASSES):
-                key = (pair, piece)
-                nc.tensor.matmul_mx(
-                    out=out, lhsT=x_codes[b, g][:, toks].bitcast(E5M2), lhsT_scale=x_scales[b, g][:, toks],
-                    rhs=w_codes[key][:, g, cols].bitcast(E4M3), rhs_scale=w_scales[key][:, g, cols],
-                    start=(g == 0), stop=(g == PASSES - 1))
+                nc.vector.quantize_mx(out=x_codes[b, g][:, toks].bitcast(E5M2), scales=x_scales[b, g][:, toks],
+                                      in_=x_side[b, t][:, g, :])
 
         qk_stage = {}
         v_stage = {}
+        rot_acc = {}
         terms = {}
 
         def open_step(s):
-            qk_stage[s] = work.tile([P, 2, 2, TT, HD], F32, name="qk_stage", bufs=5)
-            v_stage[s] = work.tile([P, 2, TT, HD], F32, name="v_stage", bufs=5)
+            qk_stage[s] = work.tile([P, 2, 2, TT, HD], F32, name="qk_stage", bufs=STAGE_BUFS)
+            v_stage[s] = work.tile([P, 2, TT, HD], F32, name="v_stage", bufs=STAGE_BUFS)
+
+        def product(out, s, t, piece, cols):
+            pair, b = divmod(s, B)
+            toks = slice(t * P, (t + 1) * P)
+            for g in range(PASSES):
+                nc.tensor.matmul_mx(
+                    out=out, lhsT=x_codes[b, g][:, toks].bitcast(E5M2), lhsT_scale=x_scales[b, g][:, toks],
+                    rhs=w_codes[pair, piece][:, g, cols].bitcast(E4M3), rhs_scale=w_scales[pair, piece][:, g, cols],
+                    start=(g == 0), stop=(g == PASSES - 1))
 
         def rest_tile(s, t):
-            pair, b = divmod(s, B)
-            acc = bank([P, 4 * REST], F32)
-            product(acc[:, 0:256], b, t, pair, "rest", slice(0, 256))
-            product(acc[:, 256:384], b, t, pair, "rest", slice(256, 384))
-            nc.vector.tensor_tensor(out=qk_stage[s][:, :, :, t, ROT:HD],
-                                    in0=acc[:].rearrange("p (r h c) -> p r h c", r=2, h=2),
-                                    in1=b_all[pair][:, 0:2, :, ROT:HD], op=ALU.add)
+            acc = bank([P, WIDTH["rest"]], F32)
+            for cols in (slice(0, REST_SPLIT), slice(REST_SPLIT, WIDTH["rest"])):
+                product(acc[:, cols], s, t, "rest", cols)
+            nc.vector.tensor_tensor(
+                out=qk_stage[s][:, :, :, t, ROT:HD], in0=acc[:].rearrange("p (r h c) -> p r h c", r=2, h=2),
+                in1=b_plain[s // B][:, 0:WIDTH["rest"]].rearrange("p (r h c) -> p r h c", r=2, h=2), op=ALU.add)
 
         def v_tiles(s, t0):
-            pair, b = divmod(s, B)
-            acc = bank([P, 2, 2 * HD], F32)
-            for dt in range(2):
-                product(acc[:, dt, :], b, t0 + dt, pair, "v", slice(0, 2 * HD))
+            acc = bank([P, 2, WIDTH["v"]], F32)
+            for i in range(2):
+                product(acc[:, i, :], s, t0 + i, "v", slice(0, WIDTH["v"]))
+            bias = b_plain[s // B][:, WIDTH["rest"]:plain_cols].rearrange("p (h c) -> p h c", h=2)
             nc.vector.tensor_tensor(out=v_stage[s][:, :, t0:t0 + 2, :].rearrange("p h t c -> p t h c"),
                                     in0=acc[:].rearrange("p t (h c) -> p t h c", h=2),
-                                    in1=b_all[pair][:, 2].unsqueeze(1).to_broadcast([P, 2, 2, HD]), op=ALU.add)
-
-        rot_acc = {}
+                                    in1=bias.unsqueeze(1).to_broadcast([P, 2, 2, HD]), op=ALU.add)
 
         def rot_product(s):
             pair, b = divmod(s, B)
-            acc = bank([P, S], F32)
-            rot_acc[s] = acc
+            rot_acc[s] = bank([P, S], F32)
             for g in range(PASSES):
-                key = (pair, "rot")
                 nc.tensor.matmul_mx(
-                    out=acc[:], lhsT=w_codes[key][:, g, :].bitcast(E4M3), lhsT_scale=w_scales[key][:, g, :],
+                    out=rot_acc[s][:], lhsT=w_codes[pair, "rot"][:, g, :].bitcast(E4M3),
+                    lhsT_scale=w_scales[pair, "rot"][:, g, :],
                     rhs=x_codes[b, g][:].bitcast(E5M2), rhs_scale=x_scales[b, g][:],
                     start=(g == 0), stop=(g == PASSES - 1))
 
-        def rot_terms(s):
+        def rot_terms_on_vector(s):
             pair = s // B
-            plain = work.tile([P, S], F32, name="plain", bufs=2)
-            nc.scalar.activation(out=plain[:], in_=rot_acc[s][:], func=ACT.Identity, bias=b_rot[:, pair:pair + 1])
-            both = work.tile([P, 2, S], F32, name="both", bufs=2)
-            terms[s] = (both[:, 0, :], both[:, 1, :])
-            nc.gpsimd.tensor_tensor(out=both[:], in0=plain[:].unsqueeze(1).to_broadcast([P, 2, S]), in1=trig[:],
+            terms[s] = work.tile([P, 2, S], F32, name="terms")
+            for i in range(2):
+                nc.vector.scalar_tensor_tensor(out=terms[s][:, i, :], in0=rot_acc[s][:],
+                                               scalar=b_rot[:, pair:pair + 1], in1=trig[:, i, :],
+                                               op0=ALU.add, op1=ALU.mult)
+
+        def rot_terms_on_gpsimd(s):
+            pair = s // B
+            biased = work.tile([P, S], F32, name="biased")
+            nc.scalar.activation(out=biased[:], in_=rot_acc[s][:], func=ACT.Identity, bias=b_rot[:, pair:pair + 1])
+            terms[s] = work.tile([P, 2, S], F32, name="terms")
+            nc.gpsimd.tensor_tensor(out=terms[s][:], in0=biased[:].unsqueeze(1).to_broadcast([P, 2, S]), in1=trig[:],
                                     op=ALU.mult)
 
-        def rot_terms_from_psum(s):
-            pair = s // B
-            both = work.tile([P, 2, S], F32, name="both", bufs=2)
-            terms[s] = (both[:, 0, :], both[:, 1, :])
-            for term, table in zip(terms[s], (cos_t, sin_t)):
-                nc.vector.scalar_tensor_tensor(out=term, in0=rot_acc[s][:], scalar=b_rot[:, pair:pair + 1],
-                                               in1=table, op0=ALU.add, op1=ALU.mult)
-
-        rot_turned = {}
-
-        def rot_finish(s):
-            by_cos, by_sin = terms[s]
+        def rot_transpose(s):
             turned = bank([P, TT, P], F32)
             for t in range(TT):
                 toks = slice(t * P, (t + 1) * P)
-                nc.tensor.matmul(turned[:, t, :], lhsT=by_cos[:, toks], rhs=ident[:], start=True, stop=False,
+                nc.tensor.matmul(turned[:, t, :], lhsT=terms[s][:, 0, toks], rhs=ident[:], start=True, stop=False,
                                  is_transpose=True)
-                nc.tensor.matmul(turned[:, t, :], lhsT=by_sin[:, toks], rhs=swap[:], start=False, stop=True,
+                nc.tensor.matmul(turned[:, t, :], lhsT=terms[s][:, 1, toks], rhs=swap[:], start=False, stop=True,
                                  is_transpose=True)
-            rot_turned[s] = turned
-
-        def rot_out(s, copy=nc.scalar.copy):
-            copy(out=qk_stage[s][:, :, :, :, 0:ROT].rearrange("p r h t c -> p (r h) t c"),
-                 in_=rot_turned[s][:].rearrange("p t (j c) -> p j t c", c=ROT))
+            nc.scalar.copy(out=qk_stage[s][:, :, :, :, 0:ROT].rearrange("p r h t c -> p (r h) t c"),
+                           in_=turned[:].rearrange("p t (n c) -> p n t c", c=ROT))
 
         def store(s, r, tiles=slice(0, TT), queue=nc.sync):
             pair, b = divmod(s, B)
-            src = v_stage[s][:] if r == 2 else qk_stage[s][:, r]
+            src = v_stage[s][:] if r == V else qk_stage[s][:, r]
             dst = outs[r][b, 2 * pair:2 * pair + 2].rearrange("h (m t) c -> m h t c", t=TT)
             queue.dma_start(out=dst[:, :, tiles, :].rearrange("m h t c -> m h (t c)"),
-                              in_=src[:, :, tiles, :].rearrange("p h t c -> p h (t c)"))
+                            in_=src[:, :, tiles, :].rearrange("p h t c -> p h (t c)"))
 
-        def interleave_pieces(pair, pieces):
-            for piece in pieces:
-                for g in range(PASSES):
-                    interleave(nc.scalar.copy, pair, g, piece)
-
-
-        tables()
-        for pair in range(PAIRS):
-            spread_bias(pair)
-        turn_bias()
-        for g in range(PASSES):
-            interleave(nc.vector.tensor_copy, 0, g, "rest")
-        quantize_piece(0, "rest")
+        interleave(nc.vector.tensor_copy, 0, "rest")
+        quantize_w(0, "rest")
         for t in range(TT):
             transpose_x(0, t)
         open_step(0)
         open_step(1)
-        for g in range(PASSES):
-            interleave(nc.vector.tensor_copy, 0, g, "rot")
+        interleave(nc.vector.tensor_copy, 0, "rot")
         quantize_x(0, 0)
         quantize_x(0, 1)
-        interleave(nc.scalar.copy, 0, 0, "v")
+        interleave(nc.scalar.copy, 0, "v", [0])
         rest_tile(0, 0)
         transpose_x(1, 0)
         transpose_x(1, 1)
-        quantize_piece(0, "rot")
+        quantize_w(0, "rot")
         quantize_x(0, 2)
         quantize_x(0, 3)
         rest_tile(0, 1)
@@ -319,90 +293,81 @@ def tile_pgtattention_pa_kernel(tc, hidden_states, W_qkv, b_qkv, out_0, out_1, o
         quantize_x(1, 0)
         rest_tile(0, 3)
         rot_product(0)
-        interleave(nc.scalar.copy, 0, 1, "v")
+        interleave(nc.scalar.copy, 0, "v", [1])
         transpose_x(1, 2)
         transpose_x(1, 3)
         quantize_x(1, 1)
-        quantize_piece(0, "v")
-        rot_terms_from_psum(0)
+        quantize_w(0, "v")
+        rot_terms_on_vector(0)
         quantize_x(1, 2)
         quantize_x(1, 3)
-        interleave_pieces(1, ("rest", "rot", "v"))
+        interleave(nc.scalar.copy, 1, "rest")
+        interleave(nc.scalar.copy, 1, "v")
+        interleave(nc.vector.tensor_copy, 1, "rot")
         v_tiles(0, 0)
         rot_product(1)
         v_tiles(0, 2)
-        store(0, 2)
-        rot_finish(0)
-        rot_terms_from_psum(1)
+        store(0, V)
+        rot_transpose(0)
+        rot_terms_on_vector(1)
         v_tiles(1, 0)
-        rot_out(0, nc.vector.tensor_copy)
-        store(0, 0)
-        store(0, 1)
+        store(0, Q)
+        store(0, K)
         v_tiles(1, 2)
-        store(1, 2)
+        store(1, V)
 
+        halves = (slice(0, TT // 2), slice(TT // 2, TT))
         for pair in range(1, PAIRS):
-            first, second = B * pair, B * pair + 1
+            before, first, second = B * pair - 1, B * pair, B * pair + 1
             more = pair + 1 < PAIRS
             for piece in ("rest", "rot", "v"):
-                quantize_piece(pair, piece)
+                quantize_w(pair, piece)
             if more:
-                for g in range(PASSES):
-                    interleave(nc.vector.tensor_copy, pair + 1, g, "rot")
-            rot_finish(first - 1)
-            rot_out(first - 1)
-            for t0 in range(0, TT, 2):
-                rest_tile(first - 1, t0)
-                rest_tile(first - 1, t0 + 1)
-                store(first - 1, 0, slice(t0, t0 + 2))
-                store(first - 1, 1, slice(t0, t0 + 2))
-                if t0 == 0:
+                interleave(nc.vector.tensor_copy, pair + 1, "rot")
+            rot_transpose(before)
+            for half in halves:
+                rest_tile(before, half.start)
+                rest_tile(before, half.start + 1)
+                if not more:
+                    store(before, Q, half)
+                    store(before, K, half)
+                if half.start == 0:
                     rot_product(first)
-                    rot_terms(first)
+                    rot_terms_on_gpsimd(first)
             if more:
-                interleave(nc.scalar.copy, pair + 1, 0, "rest")
+                store(before, Q)
+                store(before, K)
+                interleave(nc.scalar.copy, pair + 1, "rest", [0])
             open_step(first)
             open_step(second)
             v_tiles(first, 0)
             rot_product(second)
-            rot_terms(second)
+            rot_terms_on_gpsimd(second)
             v_tiles(first, 2)
-            store(first, 2)
-            if not more:
-                break
-            interleave(nc.scalar.copy, pair + 1, 1, "rest")
-            for t in range(TT):
-                rest_tile(first, t)
-            rot_finish(first)
-            rot_out(first)
-            interleave_pieces(pair + 1, ("v",))
-            v_tiles(second, 0)
-            v_tiles(second, 2)
-            store(first, 0)
-            store(first, 1)
-            store(second, 2)
+            store(first, V)
+            if more:
+                interleave(nc.scalar.copy, pair + 1, "rest", [1])
+                for t in range(TT):
+                    rest_tile(first, t)
+                rot_transpose(first)
+                interleave(nc.scalar.copy, pair + 1, "v")
+                v_tiles(second, 0)
+                v_tiles(second, 2)
+                store(first, Q)
+                store(first, K)
+                store(second, V)
 
         first, second = STEPS - 2, STEPS - 1
         v_tiles(second, 0)
         v_tiles(second, 2)
-        store(second, 2)
-        rest_tile(first, 0)
-        rest_tile(first, 1)
-        rot_finish(first)
-        rot_out(first)
-        store(first, 0, slice(0, 2))
-        store(first, 1, slice(0, 2), nc.scalar)
-        rest_tile(first, 2)
-        rest_tile(first, 3)
-        store(first, 0, slice(2, 4))
-        store(first, 1, slice(2, 4), nc.scalar)
-        rot_finish(second)
-        rot_out(second)
-        rest_tile(second, 0)
-        rest_tile(second, 1)
-        store(second, 0, slice(0, 2))
-        store(second, 1, slice(0, 2), nc.scalar)
-        rest_tile(second, 2)
-        rest_tile(second, 3)
-        store(second, 0, slice(2, 4))
-        store(second, 1, slice(2, 4), nc.scalar)
+        store(second, V)
+        for s in (first, second):
+            for half in halves:
+                if s == second and half.start == 0:
+                    rot_transpose(s)
+                rest_tile(s, half.start)
+                rest_tile(s, half.start + 1)
+                if s == first and half.start == 0:
+                    rot_transpose(s)
+                store(s, Q, half)
+                store(s, K, half, nc.scalar)

import math
from contextlib import ExitStack

import concourse.mybir as mybir
from concourse.masks import make_identity

B, S, H, NH, HD, ROT = 2, 512, 1024, 8, 128, 32
BASE = 10000.0
FLOPS = 2 * B * S * H * 3 * H

F32 = mybir.dt.float32
BF16 = mybir.dt.bfloat16
I32 = mybir.dt.int32
U32 = mybir.dt.uint32
U8 = mybir.dt.uint8
E4M3 = mybir.dt.float8_e4m3fn_x4
E5M2 = mybir.dt.float8_e5m2_x4
ALU = mybir.AluOpType
ACT = mybir.ActivationFunctionType

P = 128
PACK = 4
PASSES = H // (P * PACK)
TT = S // P
PAIRS = NH // 2
PAIR_COLS = 2 * 3 * HD
STEPS = PAIRS * B
HALF = ROT // 2
REST = HD - ROT
WIDTH = {"rot": 4 * ROT, "rest": 4 * REST, "v": 2 * HD}
REST_SPLIT = 256
RUN = 4
PSUM_BANKS = 8
STAGE_BUFS = 5
Q, K, V = 0, 1, 2


def tile_pgtattention_pa_kernel(tc, hidden_states, W_qkv, b_qkv, out_0, out_1, out_2):
    nc = tc.nc
    outs = (out_0, out_1, out_2)

    with ExitStack() as ctx:
        keep = ctx.enter_context(tc.tile_pool(name="keep", bufs=1))
        work = ctx.enter_context(tc.tile_pool(name="work", bufs=2))
        psum = ctx.enter_context(tc.psum_pool(name="psum", bufs=PSUM_BANKS))
        ctx.enter_context(tc.manual_schedule())

        def bank(shape, dtype):
            return psum.tile(shape, dtype, name="bank", tag="bank")

        b_raw = keep.tile([PAIRS, PAIR_COLS], BF16)
        nc.sync.dma_start(out=b_raw[:], in_=b_qkv.rearrange("(r c) -> r c", r=PAIRS))

        w_raw = {}
        x_raw = {}

        def load_w(pair0, count):
            for g in range(PASSES):
                raw = keep.tile([P, PACK, count * PAIR_COLS], BF16, name="w_raw_%d_%d" % (pair0, g))
                rows = W_qkv[g * P * PACK:(g + 1) * P * PACK, pair0 * PAIR_COLS:(pair0 + count) * PAIR_COLS]
                nc.sync.dma_start(out=raw[:], in_=rows.rearrange("(p j) c -> p j c", j=PACK))
                for i in range(count):
                    w_raw[pair0 + i, g] = raw[:, :, i * PAIR_COLS:(i + 1) * PAIR_COLS]

        load_w(0, 1)
        for b in range(B):
            for t in range(TT):
                raw_x = keep.tile([P, H], BF16, name="x_raw_%d_%d" % (b, t))
                nc.sync.dma_start(out=raw_x[:], in_=hidden_states[b].rearrange("(m t) k -> m t k", t=TT)[:, t, :])
                x_raw[b, t] = raw_x
        load_w(1, 1)
        load_w(2, PAIRS - 2)

        ident = keep.tile([P, P], F32)
        make_identity(nc, ident[:])
        pos = keep.tile([P, S], F32)
        nc.gpsimd.iota(pos[:], pattern=[[1, TT], [TT, P]], base=0, channel_multiplier=0,
                       allow_small_or_imprecise_dtypes=True)
        pick = keep.tile([P, PAIRS], BF16)
        nc.scalar.copy(out=pick[:], in_=ident[:, 0:PAIRS])
        swap = keep.tile([P, P], F32)
        ident_halves = ident[:].rearrange("p (n f i) -> p n f i", f=2, i=HALF)
        swap_halves = swap[:].rearrange("p (n f i) -> p n f i", f=2, i=HALF)
        for f in range(2):
            nc.scalar.copy(out=swap_halves[:, :, f, :], in_=ident_halves[:, :, 1 - f, :])

        plain_cols = WIDTH["rest"] + WIDTH["v"]
        b_rows = keep.tile([P, PAIR_COLS], BF16)
        nc.vector.memset(b_rows[:], 0.0)

        one = keep.tile([P, 1], F32)
        nc.vector.memset(one[:], 1.0)
        turns_row = keep.tile([P, 2, HALF], F32)
        for i in range(HALF):
            nc.vector.tensor_scalar(out=turns_row[:, 0, i:i + 1], in0=one[:],
                                    scalar1=BASE ** (-i / HALF) / (2 * math.pi), scalar2=None, op0=ALU.mult)
        nc.vector.tensor_scalar(out=turns_row[:, 1, :], in0=turns_row[:, 0, :], scalar1=-1.0, scalar2=None,
                                op0=ALU.mult)
        turns_diag = keep.tile([P, P // ROT, ROT], F32)
        nc.vector.tensor_tensor(
            out=turns_diag[:], in0=ident[:].rearrange("p (n c) -> p n c", c=ROT),
            in1=turns_row[:].rearrange("p f i -> p (f i)").unsqueeze(1).to_broadcast([P, P // ROT, ROT]), op=ALU.mult)
        b_parts = b_raw[:].rearrange("p (h r c) -> p r h c", h=2, r=3)
        nc.vector.tensor_copy(out=b_rows[0:PAIRS, 0:WIDTH["rest"]].rearrange("p (r h c) -> p r h c", r=2, h=2),
                              in_=b_parts[:, Q:V, :, ROT:HD])
        turns = keep.tile([P, 1], F32)
        nc.vector.tensor_reduce(out=turns[:], in_=turns_diag[:].rearrange("p n c -> p (n c)"),
                                axis=mybir.AxisListType.X, op=ALU.add)
        nc.vector.tensor_copy(out=b_rows[0:PAIRS, WIDTH["rest"]:plain_cols].rearrange("p (h c) -> p h c", h=2),
                              in_=b_parts[:, V])
        nc.vector.tensor_copy(out=b_rows[0:PAIRS, plain_cols:PAIR_COLS].rearrange("p (r h c) -> p r h c", r=2, h=2),
                              in_=b_parts[:, Q:V, :, 0:ROT])

        whole_sin = keep.tile([P, S], I32)
        whole_cos = keep.tile([P, S], I32)
        frac_sin = keep.tile([P, S], F32)
        frac_cos = keep.tile([P, S], F32)
        nc.vector.tensor_scalar(out=whole_sin[:], in0=pos[:], scalar1=turns[:], scalar2=None, op0=ALU.mult)
        nc.vector.tensor_scalar(out=whole_cos[:], in0=pos[:], scalar1=turns[:], scalar2=0.25,
                                op0=ALU.mult, op1=ALU.add)
        for frac, whole in ((frac_sin, whole_sin), (frac_cos, whole_cos)):
            nc.vector.scalar_tensor_tensor(out=frac[:], in0=pos[:], scalar=turns[:], in1=whole[:],
                                           op0=ALU.mult, op1=ALU.subtract)
        trig = keep.tile([P, 2, S], F32)
        nc.scalar.activation(out=trig[:, 1, :], in_=frac_sin[:], func=ACT.Sin, scale=2 * math.pi)
        nc.scalar.activation(out=trig[:, 0, :], in_=frac_cos[:], func=ACT.Sin, scale=2 * math.pi, bias=math.pi / 2)

        b_plain = []
        for pair in range(PAIRS):
            spread = bank([P, plain_cols], BF16)
            for cols in (slice(0, WIDTH["rest"]), slice(WIDTH["rest"], plain_cols)):
                nc.tensor.matmul(spread[:, cols], lhsT=pick[:, pair:pair + 1].to_broadcast([P, P]),
                                 rhs=b_rows[:, cols], start=True, stop=True)
            b_pair = keep.tile([P, plain_cols], BF16, name="b_plain_%d" % pair)
            nc.scalar.copy(out=b_pair[:], in_=spread[:])
            b_plain.append(b_pair)
        b_rot_psum = bank([P, PAIRS], F32)
        nc.tensor.matmul(b_rot_psum[:], lhsT=b_rows[:, plain_cols:PAIR_COLS], rhs=pick[:], start=True, stop=True)
        b_rot = keep.tile([P, PAIRS], F32)
        nc.scalar.copy(out=b_rot[:], in_=b_rot_psum[:])

        w_side = {}
        w_codes = {}
        w_scales = {}

        def interleave(copy, pair, piece, passes=range(PASSES)):
            for g in passes:
                if g == 0:
                    w_side[pair, piece] = work.tile([P, PASSES, WIDTH[piece] * PACK], BF16, name="side_" + piece,
                                                    align_bytes=64)
                side = w_side[pair, piece][:, g, :]
                src = w_raw[pair, g].rearrange("p j (h r c) -> p r h c j", h=2, r=3)
                if piece == "rot":
                    copy(out=side.rearrange("p (r h c j) -> p r h c j", r=2, h=2, j=PACK),
                         in_=src[:, Q:V, :, 0:ROT, :])
                else:
                    parts = [src[:, V]] if piece == "v" else [src[:, r, :, ROT:HD, :] for r in (Q, K)]
                    dst = side.rearrange("p (r h c i j) -> p r h c j i", r=len(parts), h=2, i=RUN, j=PACK)
                    for r, part in enumerate(parts):
                        copy(out=dst[:, r], in_=part.rearrange("p h (c i) j -> p h c j i", i=RUN))

        def quantize_w(pair, piece):
            key = (pair, piece)
            w_codes[key] = keep.tile([P, PASSES, WIDTH[piece]], U32, name="w_codes_%d_%s" % key, align_bytes=64)
            w_scales[key] = keep.tile([P, PASSES, WIDTH[piece]], U8, name="w_scales_%d_%s" % key, align_bytes=64)
            spans = [slice(g, g + 1) for g in range(PASSES)] if piece == "rest" else [slice(0, PASSES)]
            for span in spans:
                nc.vector.quantize_mx(out=w_codes[key][:, span, :].rearrange("p g c -> p (g c)").bitcast(E4M3),
                                      scales=w_scales[key][:, span, :].rearrange("p g c -> p (g c)"),
                                      in_=w_side[key][:, span, :].rearrange("p g c -> p (g c)"))

        x_side = {}
        x_codes = {}
        x_scales = {}
        for b in range(B):
            for g in range(PASSES):
                x_codes[b, g] = keep.tile([P, S], U32, name="x_codes_%d_%d" % (b, g), align_bytes=64)
                x_scales[b, g] = keep.tile([P, S], U8, name="x_scales_%d_%d" % (b, g), align_bytes=64)

        def transpose_x(b, t):
            words = x_raw[b, t][:].bitcast(F32)
            turned = bank([P, PASSES, 2, P], F32)
            for g in range(PASSES):
                for u in range(2):
                    nc.tensor.transpose(turned[:, g, u, :], words[:, 2 * P * g + u:2 * P * (g + 1):2], ident[:])
            x_side[b, t] = work.tile([P, PASSES, P * PACK], BF16, name="side_x", bufs=TT, align_bytes=64)
            nc.scalar.copy(out=x_side[b, t][:].bitcast(F32).rearrange("p g (m u) -> p g m u", u=2),
                           in_=turned[:].rearrange("p g u m -> p g m u"))

        def quantize_x(b, t):
            toks = slice(t * P, (t + 1) * P)
            for g in range(PASSES):
                nc.vector.quantize_mx(out=x_codes[b, g][:, toks].bitcast(E5M2), scales=x_scales[b, g][:, toks],
                                      in_=x_side[b, t][:, g, :])

        qk_stage = {}
        v_stage = {}
        rot_acc = {}
        terms = {}

        def open_step(s):
            qk_stage[s] = work.tile([P, 2, 2, TT, HD], F32, name="qk_stage", bufs=STAGE_BUFS)
            v_stage[s] = work.tile([P, 2, TT, HD], F32, name="v_stage", bufs=STAGE_BUFS)

        def product(out, s, t, piece, cols):
            pair, b = divmod(s, B)
            toks = slice(t * P, (t + 1) * P)
            for g in range(PASSES):
                nc.tensor.matmul_mx(
                    out=out, lhsT=x_codes[b, g][:, toks].bitcast(E5M2), lhsT_scale=x_scales[b, g][:, toks],
                    rhs=w_codes[pair, piece][:, g, cols].bitcast(E4M3), rhs_scale=w_scales[pair, piece][:, g, cols],
                    start=(g == 0), stop=(g == PASSES - 1))

        def rest_tile(s, t):
            acc = bank([P, WIDTH["rest"]], F32)
            for cols in (slice(0, REST_SPLIT), slice(REST_SPLIT, WIDTH["rest"])):
                product(acc[:, cols], s, t, "rest", cols)
            nc.vector.tensor_tensor(
                out=qk_stage[s][:, :, :, t, ROT:HD], in0=acc[:].rearrange("p (r h c) -> p r h c", r=2, h=2),
                in1=b_plain[s // B][:, 0:WIDTH["rest"]].rearrange("p (r h c) -> p r h c", r=2, h=2), op=ALU.add)

        def v_tiles(s, t0):
            acc = bank([P, 2, WIDTH["v"]], F32)
            for i in range(2):
                product(acc[:, i, :], s, t0 + i, "v", slice(0, WIDTH["v"]))
            bias = b_plain[s // B][:, WIDTH["rest"]:plain_cols].rearrange("p (h c) -> p h c", h=2)
            nc.vector.tensor_tensor(out=v_stage[s][:, :, t0:t0 + 2, :].rearrange("p h t c -> p t h c"),
                                    in0=acc[:].rearrange("p t (h c) -> p t h c", h=2),
                                    in1=bias.unsqueeze(1).to_broadcast([P, 2, 2, HD]), op=ALU.add)

        def rot_product(s):
            pair, b = divmod(s, B)
            rot_acc[s] = bank([P, S], F32)
            for g in range(PASSES):
                nc.tensor.matmul_mx(
                    out=rot_acc[s][:], lhsT=w_codes[pair, "rot"][:, g, :].bitcast(E4M3),
                    lhsT_scale=w_scales[pair, "rot"][:, g, :],
                    rhs=x_codes[b, g][:].bitcast(E5M2), rhs_scale=x_scales[b, g][:],
                    start=(g == 0), stop=(g == PASSES - 1))

        def rot_terms_on_vector(s):
            pair = s // B
            terms[s] = work.tile([P, 2, S], F32, name="terms")
            for i in range(2):
                nc.vector.scalar_tensor_tensor(out=terms[s][:, i, :], in0=rot_acc[s][:],
                                               scalar=b_rot[:, pair:pair + 1], in1=trig[:, i, :],
                                               op0=ALU.add, op1=ALU.mult)

        def rot_terms_on_gpsimd(s):
            pair = s // B
            biased = work.tile([P, S], F32, name="biased")
            nc.scalar.activation(out=biased[:], in_=rot_acc[s][:], func=ACT.Identity, bias=b_rot[:, pair:pair + 1])
            terms[s] = work.tile([P, 2, S], F32, name="terms")
            nc.gpsimd.tensor_tensor(out=terms[s][:], in0=biased[:].unsqueeze(1).to_broadcast([P, 2, S]), in1=trig[:],
                                    op=ALU.mult)

        def rot_transpose(s):
            turned = bank([P, TT, P], F32)
            for t in range(TT):
                toks = slice(t * P, (t + 1) * P)
                nc.tensor.matmul(turned[:, t, :], lhsT=terms[s][:, 0, toks], rhs=ident[:], start=True, stop=False,
                                 is_transpose=True)
                nc.tensor.matmul(turned[:, t, :], lhsT=terms[s][:, 1, toks], rhs=swap[:], start=False, stop=True,
                                 is_transpose=True)
            nc.scalar.copy(out=qk_stage[s][:, :, :, :, 0:ROT].rearrange("p r h t c -> p (r h) t c"),
                           in_=turned[:].rearrange("p t (n c) -> p n t c", c=ROT))

        def store(s, r, tiles=slice(0, TT), queue=nc.sync):
            pair, b = divmod(s, B)
            src = v_stage[s][:] if r == V else qk_stage[s][:, r]
            dst = outs[r][b, 2 * pair:2 * pair + 2].rearrange("h (m t) c -> m h t c", t=TT)
            queue.dma_start(out=dst[:, :, tiles, :].rearrange("m h t c -> m h (t c)"),
                            in_=src[:, :, tiles, :].rearrange("p h t c -> p h (t c)"))

        interleave(nc.vector.tensor_copy, 0, "rest")
        quantize_w(0, "rest")
        for t in range(TT):
            transpose_x(0, t)
        open_step(0)
        open_step(1)
        interleave(nc.vector.tensor_copy, 0, "rot")
        quantize_x(0, 0)
        quantize_x(0, 1)
        interleave(nc.scalar.copy, 0, "v", [0])
        rest_tile(0, 0)
        transpose_x(1, 0)
        transpose_x(1, 1)
        quantize_w(0, "rot")
        quantize_x(0, 2)
        quantize_x(0, 3)
        rest_tile(0, 1)
        rest_tile(0, 2)
        quantize_x(1, 0)
        rest_tile(0, 3)
        rot_product(0)
        interleave(nc.scalar.copy, 0, "v", [1])
        transpose_x(1, 2)
        transpose_x(1, 3)
        quantize_x(1, 1)
        quantize_w(0, "v")
        rot_terms_on_vector(0)
        quantize_x(1, 2)
        quantize_x(1, 3)
        interleave(nc.scalar.copy, 1, "rest")
        interleave(nc.scalar.copy, 1, "v")
        interleave(nc.vector.tensor_copy, 1, "rot")
        v_tiles(0, 0)
        rot_product(1)
        v_tiles(0, 2)
        store(0, V)
        rot_transpose(0)
        rot_terms_on_vector(1)
        v_tiles(1, 0)
        store(0, Q)
        store(0, K)
        v_tiles(1, 2)
        store(1, V)

        halves = (slice(0, TT // 2), slice(TT // 2, TT))
        for pair in range(1, PAIRS):
            before, first, second = B * pair - 1, B * pair, B * pair + 1
            more = pair + 1 < PAIRS
            for piece in ("rest", "rot", "v"):
                quantize_w(pair, piece)
            if more:
                interleave(nc.vector.tensor_copy, pair + 1, "rot")
            rot_transpose(before)
            for half in halves:
                rest_tile(before, half.start)
                rest_tile(before, half.start + 1)
                if not more:
                    store(before, Q, half)
                    store(before, K, half)
                if half.start == 0:
                    rot_product(first)
                    rot_terms_on_gpsimd(first)
            if more:
                store(before, Q)
                store(before, K)
                interleave(nc.scalar.copy, pair + 1, "rest", [0])
            open_step(first)
            open_step(second)
            v_tiles(first, 0)
            rot_product(second)
            rot_terms_on_gpsimd(second)
            v_tiles(first, 2)
            store(first, V)
            if more:
                interleave(nc.scalar.copy, pair + 1, "rest", [1])
                for t in range(TT):
                    rest_tile(first, t)
                rot_transpose(first)
                interleave(nc.scalar.copy, pair + 1, "v")
                v_tiles(second, 0)
                v_tiles(second, 2)
                store(first, Q)
                store(first, K)
                store(second, V)

        first, second = STEPS - 2, STEPS - 1
        v_tiles(second, 0)
        v_tiles(second, 2)
        store(second, V)
        for s in (first, second):
            for half in halves:
                if s == second and half.start == 0:
                    rot_transpose(s)
                rest_tile(s, half.start)
                rest_tile(s, half.start + 1)
                if s == first and half.start == 0:
                    rot_transpose(s)
                store(s, Q, half)
                store(s, K, half, nc.scalar)
